import numpy as np
import ml_dtypes


def mxq(x, axis, fmt="e4m3"):
    dtype, down = {"e4m3": (ml_dtypes.float8_e4m3fn, 7), "e5m2": (ml_dtypes.float8_e5m2, 14)}[fmt]
    v = np.moveaxis(np.asarray(x, np.float32).astype(ml_dtypes.bfloat16).astype(np.float64), axis, -1)
    blocks = v.reshape(v.shape[:-1] + (-1, 32))
    amax = np.abs(blocks).max(-1, keepdims=True)
    byte = np.maximum(np.where(amax > 0, np.frexp(amax)[1] - 1 + 127, 0) - down, 1)
    scale = np.exp2(byte - 127.0)
    codes = (blocks / scale).astype(np.float32).astype(dtype).astype(np.float64)
    return np.moveaxis((codes * scale).reshape(v.shape), -1, axis)


WIDE = False


def mx_kscale(k):
    if not WIDE:
        return np.ones(k)
    levels = np.array([10, -10, 5, -5, 0])
    a = np.random.permutation(np.resize(levels, k // 512 * 4)).reshape(k // 512, 4)
    idx = np.arange(k)
    return np.exp2(a[idx // 512, idx % 128 // 32])


BF16 = ml_dtypes.bfloat16


def bf(x):
    return np.asarray(x, np.float32).astype(BF16)


def f64(x):
    return np.asarray(x).astype(np.float64)


T, M, HW, D, DK, H = 2, 512, 768, 1024, 1024, 8
DH = DK // H
DV = D // H
SIGMA = 0.5
EXTENT = 27.0


def rope_2d(x, pos):
    nt, n, c = x.shape
    half, quarter = c // 2, c // 4
    theta = 100.0 ** (-2.0 * np.arange(quarter) / half)

    def apply(part, p):
        fr = p[..., None] * theta
        cos, sin = np.cos(fr), np.sin(fr)
        pr = part.reshape(nt, n, quarter, 2)
        x1, x2 = pr[..., 0], pr[..., 1]
        return np.stack([x1 * cos - x2 * sin, x1 * sin + x2 * cos], axis=-1).reshape(nt, n, half)

    return np.concatenate([apply(x[:, :, :half], pos[..., 0]), apply(x[:, :, half:], pos[..., 1])], axis=-1)


def setup_inputs():
    t = np.repeat(mx_kscale(D)[::2], 2)
    return {"q_norm": bf(np.random.standard_normal((T, HW, DK))),
            "k_norm": bf(np.random.standard_normal((T, M, DK))),
            "updated_track_tokens": bf(np.random.standard_normal((T, M, D)) * t),
            "tracks": bf(np.random.uniform(0.0, EXTENT, (T, M, 2))),
            "feature_positions": bf(np.random.uniform(0.0, EXTENT, (HW, 2))),
            "W_out": bf(np.random.standard_normal((D, D)) / np.sqrt(D) / t)}


def reference(q_norm, k_norm, updated_track_tokens, tracks, feature_positions, W_out):
    tr = f64(tracks)
    qh = f64(q_norm).reshape(T, HW, H, DH).transpose(0, 2, 1, 3)
    kh = f64(k_norm).reshape(T, M, H, DH).transpose(0, 2, 1, 3)
    vh = rope_2d(f64(updated_track_tokens), tr).reshape(T, M, H, DV).transpose(0, 2, 1, 3)
    scores = qh @ kh.transpose(0, 1, 3, 2) / np.sqrt(DH)
    diff = f64(feature_positions)[None, :, None, :] - tr[:, None, :, :]
    d2 = np.sum(diff * diff, axis=-1)
    bias = -d2 / (2.0 * SIGMA ** 2)
    scores = scores + bias[:, None, :, :]
    e = np.exp(scores - scores.max(-1, keepdims=True))
    sampled = (mxq(e, 3, "e4m3") @ mxq(vh, 2, "e4m3")) / e.sum(-1, keepdims=True)
    sampled = sampled.transpose(0, 2, 1, 3).reshape(T, HW, D)
    return mxq(sampled, 2, "e4m3") @ mxq(f64(W_out), 1, "e4m3").T

@@ -1,0 +1,451 @@
+import math
+from contextlib import ExitStack
+
+import concourse.mybir as mybir
+from concourse.masks import make_identity
+
+F32 = mybir.dt.float32
+BF16 = mybir.dt.bfloat16
+U32 = mybir.dt.uint32
+U8 = mybir.dt.uint8
+FP8X4 = mybir.dt.float8_e4m3fn_x4
+ALU = mybir.AluOpType
+ACT = mybir.ActivationFunctionType
+AX = mybir.AxisListType
+
+P = 128
+T = 2
+M = 512
+HW = 768
+D = 1024
+H = 8
+DH = D // H
+IT = HW // P
+JB = M // P
+ROUNDS = T * IT
+PAIRS = 256
+SLOTS = 4
+
+SCALE = 1.0 / math.sqrt(DH)
+BIAS_GAIN = 2.0 / SCALE
+TURN = 2.0 * math.pi
+ROUND_MAGIC = 12582912.0
+
+FLOPS = 2 * (2 * T * H * HW * M * DH) + 2 * T * HW * D * D
+
+
+def cols(index, width):
+    return slice(index * width, (index + 1) * width)
+
+
+def tile_attentionalsplatting_pb_kernel(
+    tc, q_norm, k_norm, updated_track_tokens, tracks, feature_positions, W_out, out
+):
+    nc = tc.nc
+    with ExitStack() as stack:
+        stack.enter_context(tc.manual_schedule())
+        const = stack.enter_context(tc.tile_pool(name="const", bufs=1))
+        q_pool = stack.enter_context(tc.tile_pool(name="q_pool", bufs=4))
+        keep = stack.enter_context(tc.tile_pool(name="keep", bufs=1))
+        values = stack.enter_context(tc.tile_pool(name="values", bufs=1))
+        stats = stack.enter_context(tc.tile_pool(name="stats", bufs=6))
+        psum_s = stack.enter_context(tc.psum_pool(name="psum_s", bufs=4))
+        psum_t = stack.enter_context(tc.psum_pool(name="psum_t", bufs=2))
+        psum_m = stack.enter_context(tc.psum_pool(name="psum_m", bufs=2))
+
+        trk_j = const.tile([P, T * JB, 2], BF16)
+        trk_v = const.tile([P, T, SLOTS, 2], BF16)
+        fpos = const.tile([P, 2 * HW], BF16)
+        with nc.allow_non_contiguous_dma(reason="a few KiB of positions"):
+            nc.scalar.dma_start(out=trk_j[:], in_=tracks.rearrange("t (jb p) c -> p (t jb) c", p=P))
+            nc.scalar.dma_start(
+                out=trk_v[:].rearrange("p t (u e) c -> p (t u) (e c)", u=2),
+                in_=tracks.rearrange("t (u p e) c -> p (t u) (e c)", u=2, p=P),
+            )
+            nc.scalar.dma_start(
+                out=fpos[:], in_=feature_positions.rearrange("i c -> (i c)").partition_broadcast(P)
+            )
+
+        q_tiles = {}
+
+        def load_q(r):
+            if r < ROUNDS:
+                q_tiles[r] = q_pool.tile([P, D], BF16, tag="q_sb", name="q_sb%d" % r)
+                nc.sync.dma_start(out=q_tiles[r][:], in_=q_norm[r // IT, cols(r % IT, P), :])
+
+        tok = [values.tile([P, SLOTS, D], BF16, name="tok%d" % t) for t in range(T)]
+
+        def load_tok(t):
+            nc.sync.dma_start(
+                out=tok[t][:].rearrange("p (u e) c -> p u (e c)", u=2),
+                in_=updated_track_tokens[t].rearrange("(u p e) c -> p u (e c)", u=2, p=P),
+            )
+
+        bias_t = [keep.tile([P, JB, HW], F32, name="bias_t%d" % t) for t in range(T)]
+        k_t = [keep.tile([P, H, M], BF16, name="k_t%d" % t) for t in range(T)]
+        v_codes = [keep.tile([P, D], U32, name="v_codes%d" % t, align_bytes=64) for t in range(T)]
+        v_scales = [keep.tile([P, D], U8, name="v_scales%d" % t, align_bytes=64) for t in range(T)]
+        w_codes = keep.tile([P, 2, D], U32, align_bytes=64)
+        w_scales = keep.tile([P, 2, D], U8, align_bytes=64)
+        q_t = {}
+        v_grouped = {}
+
+        ident_bf = const.tile([P, P], BF16)
+        ident_f = const.tile([P, P], F32)
+
+        def transpose_q(r):
+            qt_ps = psum_t.tile([P, H, P], BF16, tag="tp", name="qt_ps")
+            for h in range(H):
+                nc.tensor.transpose(out=qt_ps[:, h, :], in_=q_tiles[r][:, cols(h, DH)], identity=ident_bf[:])
+            return qt_ps
+
+        with tc.tile_pool(name="prep", bufs=1) as prep:
+            k_sb = {}
+
+            def load_k(t):
+                k_sb[t] = prep.tile([P, JB, D], BF16, tag="k_sb", name="k_sb%d" % t)
+                nc.sync.dma_start(out=k_sb[t][:], in_=k_norm[t].rearrange("(jb p) c -> p jb c", p=P))
+
+            w_sb = prep.tile([P, D // P, D], BF16)
+            load_k(0)
+            load_q(0)
+            load_tok(0)
+            nc.sync.dma_start(out=w_sb[:], in_=W_out.rearrange("(ob p) c -> p ob c", p=P))
+            load_tok(1)
+            load_q(1)
+            load_q(2)
+            load_q(3)
+
+            make_identity(nc, ident_bf[:])
+            make_identity(nc, ident_f[:])
+
+            theta = const.tile([P, PAIRS], F32)
+            nc.vector.memset(theta[:, 0:1], 1.0)
+            for doubling in range(8):
+                width = 2**doubling
+                nc.vector.tensor_scalar_mul(
+                    out=theta[:, width : 2 * width], in0=theta[:, 0:width], scalar1=100.0 ** (-width / PAIRS)
+                )
+            neg_trk = const.tile([P, T * JB, 2], F32)
+            nc.vector.tensor_scalar_mul(out=neg_trk[:], in0=trk_j[:], scalar1=-1.0)
+            turns = const.tile([P, T, 2, SLOTS], F32)
+            nc.vector.tensor_scalar_mul(
+                out=turns[:], in0=trk_v[:].rearrange("p t s c -> p t c s"), scalar1=1.0 / TURN
+            )
+            quarter = const.tile([P, 1], F32)
+            nc.vector.memset(quarter[:], 1.0)
+            nc.vector.tensor_scalar_mul(out=quarter[:], in0=quarter[:], scalar1=math.pi / 2.0)
+            fxy = fpos[:].rearrange("p (i c) -> p c i", c=2)
+            squares = {}
+
+            def square_distances(t, jb):
+                for c in range(2):
+                    squares[t, jb, c] = prep.tile([P, HW], F32, tag="square%d" % c, name="square%d" % c, bufs=2)
+                    nc.scalar.activation(
+                        out=squares[t, jb, c][:],
+                        in_=fxy[:, c, :],
+                        func=ACT.Square,
+                        bias=neg_trk[:, t * JB + jb, c : c + 1],
+                        scale=1.0,
+                    )
+
+            def finish_bias(t, jb):
+                dx2, dy2 = squares[t, jb, 0], squares[t, jb, 1]
+                nc.vector.tensor_tensor(out=dx2[:], in0=dx2[:], in1=dy2[:], op=ALU.add)
+                nc.vector.tensor_scalar_mul(out=bias_t[t][:, jb, :], in0=dx2[:], scalar1=-BIAS_GAIN)
+
+            def transpose_keys(t, hp):
+                kt_ps = psum_t.tile([P, 2, JB, P], BF16, tag="tp", name="kt_ps")
+                for hh in range(2):
+                    for jb in range(JB):
+                        nc.tensor.transpose(
+                            out=kt_ps[:, hh, jb, :], in_=k_sb[t][:, jb, cols(2 * hp + hh, DH)], identity=ident_bf[:]
+                        )
+                nc.vector.tensor_copy(
+                    out=k_t[t][:, 2 * hp : 2 * hp + 2, :].rearrange("p h (jb j) -> p h jb j", jb=JB), in_=kt_ps[:]
+                )
+
+            table = {}
+
+            def angle_tables(t, half):
+                shape = [P, PAIRS, SLOTS]
+                u = prep.tile(shape, F32, tag="u")
+                nc.vector.tensor_tensor(
+                    out=u[:],
+                    in0=theta[:].unsqueeze(2).to_broadcast(shape),
+                    in1=turns[:, t, half, :].unsqueeze(1).to_broadcast(shape),
+                    op=ALU.mult,
+                )
+                back = prep.tile(shape, F32, tag="back")
+                nc.vector.tensor_scalar_add(out=back[:], in0=u[:], scalar1=ROUND_MAGIC)
+                nc.vector.scalar_tensor_tensor(
+                    out=back[:], in0=back[:], scalar=ROUND_MAGIC, in1=u[:], op0=ALU.subtract, op1=ALU.subtract
+                )
+                fold = prep.tile(shape, F32, tag="fold")
+                nc.vector.scalar_tensor_tensor(
+                    out=fold[:], in0=back[:], scalar=-1.0, in1=back[:], op0=ALU.mult, op1=ALU.min
+                )
+                table[t, half] = values.tile([P, 3, PAIRS, SLOTS], F32, name="table%d%d" % (t, half))
+                nc.scalar.activation(
+                    out=table[t, half][:, 1, :, :], in_=fold[:], func=ACT.Sin, bias=quarter[:, 0:1], scale=TURN
+                )
+                nc.scalar.activation(out=table[t, half][:, 2, :, :], in_=back[:], func=ACT.Sin, scale=-TURN)
+
+            def rotate_values(t, half):
+                tab = table[t, half]
+                nc.gpsimd.tensor_scalar(
+                    out=tab[:, 0, :, :], in0=tab[:, 2, :, :], scalar1=-1.0, scalar2=0.0, op0=ALU.mult, op1=ALU.add
+                )
+                ab = tok[t][:, :, cols(half, 2 * PAIRS)].rearrange("p s (i w) -> p w i s", w=2)
+                full = [P, PAIRS, 2, SLOTS]
+                part_a = values.tile(full, F32, tag="part_a")
+                part_b = values.tile(full, F32, tag="part_b")
+                nc.gpsimd.tensor_tensor(
+                    out=part_a[:],
+                    in0=ab[:, 0, :, :].unsqueeze(2).to_broadcast(full),
+                    in1=tab[:, 1:3, :, :].rearrange("p w i s -> p i w s"),
+                    op=ALU.mult,
+                )
+                nc.gpsimd.tensor_tensor(
+                    out=part_b[:],
+                    in0=ab[:, 1, :, :].unsqueeze(2).to_broadcast(full),
+                    in1=tab[:, 0:2, :, :].rearrange("p w i s -> p i w s"),
+                    op=ALU.mult,
+                )
+                v_grouped[t, half] = values.tile(full, BF16, name="v_grouped%d%d" % (t, half), align_bytes=64)
+                nc.gpsimd.tensor_tensor(out=v_grouped[t, half][:], in0=part_a[:], in1=part_b[:], op=ALU.add)
+
+            def quantise_weights(g):
+                w_grouped = prep.tile([P, D, 2], F32, tag="w_grouped", align_bytes=64)
+                for op in range(4):
+                    wt_ps = psum_t.tile([P, 2, 2, P], F32, tag="tp", name="wt_ps")
+                    for u in range(2):
+                        for ob in range(2):
+                            nc.tensor.transpose(
+                                out=wt_ps[:, u, ob, :],
+                                in_=w_sb[:, 2 * op + ob, :].bitcast(F32)[:, cols(2 * g + u, P)],
+                                identity=ident_f[:],
+                            )
+                    nc.scalar.copy(
+                        out=w_grouped[:, cols(op, 2 * P), :], in_=wt_ps[:].rearrange("p u ob o -> p (ob o) u")
+                    )
+                nc.vector.quantize_mx(
+                    out=w_codes[:, g, :].bitcast(FP8X4),
+                    scales=w_scales[:, g, :],
+                    in_=w_grouped[:].rearrange("p o u -> p (o u)").bitcast(BF16),
+                )
+
+            for t in range(T):
+                square_distances(t, 0)
+                square_distances(t, 1)
+                angle_tables(t, 0)
+                rotate_values(t, 0)
+                finish_bias(t, 0)
+                finish_bias(t, 1)
+                square_distances(t, 2)
+                square_distances(t, 3)
+                angle_tables(t, 1)
+                rotate_values(t, 1)
+                finish_bias(t, 2)
+                finish_bias(t, 3)
+                for hp in range(H // 2):
+                    transpose_keys(t, hp)
+                if t + 1 < T:
+                    load_k(t + 1)
+            for g in range(2):
+                quantise_weights(g)
+
+        work = stack.enter_context(tc.tile_pool(name="work", bufs=2))
+        sc_of, shift_of, e_of, et_of, eg_of = {}, {}, {}, {}, {}
+        rowsum_of, codes_of, scales_of, pv_of, sampled_of, st_of, sg_of, po_of = {}, {}, {}, {}, {}, {}, {}, {}
+
+        def copy_q(r, qt_ps):
+            q_t[r] = work.tile([P, H, P], BF16, tag="q_t", name="q_t")
+            nc.scalar.copy(out=q_t[r][:], in_=qt_ps[:])
+
+        def scores(n):
+            r, h = divmod(n, H)
+            t, it = divmod(r, IT)
+            sc_of[n] = psum_s.tile([P, M], F32, tag="sc", name="sc")
+            for jb in range(JB):
+                nc.tensor.matmul(
+                    out=sc_of[n][:, cols(jb, P)],
+                    lhsT=bias_t[t][:, jb, cols(it, P)],
+                    rhs=ident_f[:],
+                    is_transpose=True,
+                    start=(jb == 0),
+                    stop=False,
+                )
+            nc.tensor.matmul(out=sc_of[n][:], lhsT=q_t[r][:, h, :], rhs=k_t[t][:, h, :], start=False, stop=True)
+
+        def row_max(n):
+            top = stats.tile([P, 1], F32, tag="top")
+            nc.vector.tensor_reduce(out=top[:], in_=sc_of[n][:], axis=AX.X, op=ALU.max)
+            return top
+
+        def row_shift(n, top):
+            shift_of[n] = stats.tile([P, 1], F32, tag="shift", name="shift")
+            nc.vector.tensor_scalar_mul(out=shift_of[n][:], in0=top[:], scalar1=-SCALE)
+
+        def exponent(n):
+            r, h = divmod(n, H)
+            if h == 0:
+                rowsum_of[r] = stats.tile([P, H], F32, tag="rowsum", name="rowsum")
+            if n % 2 == 0:
+                e_of[n // 2] = work.tile([P, 2, M], BF16, tag="e_sb", name="e_sb", bufs=3)
+            nc.scalar.activation(
+                out=e_of[n // 2][:, n % 2, :],
+                in_=sc_of[n][:],
+                func=ACT.Exp,
+                bias=shift_of[n][:],
+                scale=SCALE,
+                accum_out=rowsum_of[r][:, h : h + 1],
+            )
+
+        def transpose_e(m):
+            et_of[m] = psum_t.tile([P, 2, 2, P], F32, tag="tp", name="et_ps")
+            for hh in range(2):
+                for u in range(2):
+                    nc.tensor.transpose(
+                        out=et_of[m][:, hh, u, :],
+                        in_=e_of[m][:, hh, :].bitcast(F32)[:, cols(u, P)],
+                        identity=ident_f[:],
+                    )
+
+        def regroup_e(m):
+            eg_of[m] = work.tile([P, 2, P, 2], F32, tag="e_grouped", name="e_grouped", bufs=3, align_bytes=64)
+            if m % 2 == 0:
+                nc.vector.tensor_copy(out=eg_of[m][:], in_=et_of[m][:].rearrange("p h u i -> p h i u"))
+            else:
+                nc.scalar.copy(out=eg_of[m][:], in_=et_of[m][:].rearrange("p h u i -> p h i u"))
+
+        def quantise_e(m):
+            r, hp = divmod(m, H // 2)
+            if hp == 0:
+                codes_of[r] = work.tile([P, H * P], U32, tag="e_codes", name="e_codes", align_bytes=64)
+                scales_of[r] = work.tile([P, H * P], U8, tag="e_scales", name="e_scales", align_bytes=64)
+            nc.vector.quantize_mx(
+                out=codes_of[r][:, cols(hp, 2 * P)].bitcast(FP8X4),
+                scales=scales_of[r][:, cols(hp, 2 * P)],
+                in_=eg_of[m][:].rearrange("p h i u -> p (h i u)").bitcast(BF16),
+            )
+
+        def quantise_values(t):
+            for half in range(2):
+                nc.vector.quantize_mx(
+                    out=v_codes[t][:, cols(half, 2 * PAIRS)].bitcast(FP8X4),
+                    scales=v_scales[t][:, cols(half, 2 * PAIRS)],
+                    in_=v_grouped[t, half][:].rearrange("p i w s -> p (i w s)"),
+                )
+
+        def multiply_values(r):
+            t = r // IT
+            for half in range(2):
+                pv_of[r, half] = psum_m.tile([P, 4, DH], F32, tag="mm", name="pv")
+                for hq in range(4):
+                    h = 4 * half + hq
+                    nc.tensor.matmul_mx(
+                        out=pv_of[r, half][:, hq, :],
+                        lhsT=codes_of[r][:, cols(h, P)].bitcast(FP8X4),
+                        lhsT_scale=scales_of[r][:, cols(h, P)],
+                        rhs=v_codes[t][:, cols(h, DH)].bitcast(FP8X4),
+                        rhs_scale=v_scales[t][:, cols(h, DH)],
+                        start=True,
+                        stop=True,
+                    )
+
+        def normalise(r):
+            inv_sum = stats.tile([P, H], F32, tag="inv_sum")
+            nc.vector.reciprocal(out=inv_sum[:], in_=rowsum_of[r][:])
+            sampled_of[r] = work.tile([P, 2, 4, DH], BF16, tag="sampled", name="sampled")
+            for half in range(2):
+                nc.vector.tensor_tensor(
+                    out=sampled_of[r][:, half, :, :],
+                    in0=pv_of[r, half][:],
+                    in1=inv_sum[:, cols(half, 4)].unsqueeze(2).to_broadcast([P, 4, DH]),
+                    op=ALU.mult,
+                )
+
+        def transpose_sampled(r):
+            st_of[r] = psum_t.tile([P, 2, 2, P], F32, tag="tp", name="st_ps")
+            words = sampled_of[r][:].rearrange("p a b c -> p (a b c)").bitcast(F32)
+            for g in range(2):
+                for u in range(2):
+                    nc.tensor.transpose(out=st_of[r][:, g, u, :], in_=words[:, cols(2 * g + u, P)], identity=ident_f[:])
+
+        def regroup_sampled(r):
+            sg_of[r] = work.tile([P, 2, P, 2], F32, tag="s_grouped", name="s_grouped", align_bytes=64)
+            nc.scalar.copy(out=sg_of[r][:], in_=st_of[r][:].rearrange("p g u i -> p g i u"))
+
+        def quantise_sampled(r):
+            s_codes = work.tile([P, 2 * P], U32, tag="s_codes", align_bytes=64)
+            s_scales = work.tile([P, 2 * P], U8, tag="s_scales", align_bytes=64)
+            nc.vector.quantize_mx(
+                out=s_codes[:].bitcast(FP8X4),
+                scales=s_scales[:],
+                in_=sg_of[r][:].rearrange("p g i u -> p (g i u)").bitcast(BF16),
+            )
+            sg_of[r] = (s_codes, s_scales)
+
+        def project(r):
+            s_codes, s_scales = sg_of[r]
+            for nh in range(2):
+                po_of[r, nh] = psum_m.tile([P, 512], F32, tag="mm", name="po")
+                for g in range(2):
+                    nc.tensor.matmul_mx(
+                        out=po_of[r, nh][:],
+                        lhsT=s_codes[:, cols(g, P)].bitcast(FP8X4),
+                        lhsT_scale=s_scales[:, cols(g, P)],
+                        rhs=w_codes[:, g, cols(nh, 512)].bitcast(FP8X4),
+                        rhs_scale=w_scales[:, g, cols(nh, 512)],
+                        start=(g == 0),
+                        stop=(g == 1),
+                    )
+
+        def store(r):
+            t, it = divmod(r, IT)
+            o_sb = work.tile([P, D], F32, tag="o_sb")
+            for nh in range(2):
+                nc.scalar.copy(out=o_sb[:, cols(nh, 512)], in_=po_of[r, nh][:])
+            nc.sync.dma_start(out=out[t, cols(it, P), :], in_=o_sb[:])
+
+        heads = ROUNDS * H
+        copy_q(0, transpose_q(0))
+        load_q(4)
+        next_q = {}
+        for n in range(heads + 20):
+            if n >= 4 and n % 2 == 0 and (n - 4) // 2 < heads // 2:
+                transpose_e((n - 4) // 2)
+            r, step = divmod(n, H)
+            if step == 5 and r + 1 < ROUNDS:
+                next_q[r + 1] = transpose_q(r + 1)
+                load_q(r + 5)
+            if step == 7 and 0 <= r - 1 < ROUNDS:
+                transpose_sampled(r - 1)
+            if n < heads:
+                scores(n)
+            if step == 5 and 0 <= r - 1 < ROUNDS:
+                multiply_values(r - 1)
+            if step == 2 and 0 <= r - 2 < ROUNDS:
+                project(r - 2)
+            top = row_max(n - 1) if 0 <= n - 1 < heads else None
+            if 0 <= n - 2 < heads:
+                exponent(n - 2)
+            if n >= 5 and n % 2 == 1 and (n - 5) // 2 < heads // 2:
+                regroup_e((n - 5) // 2)
+            if n >= 6 and n % 2 == 0 and (n - 6) // 2 < heads // 2:
+                quantise_e((n - 6) // 2)
+            if step == 3 and 0 <= r - 1 < ROUNDS and (r - 1) % IT == 0:
+                quantise_values((r - 1) // IT)
+            if step == 6 and r + 1 < ROUNDS:
+                copy_q(r + 1, next_q[r + 1])
+            if step == 6 and 0 <= r - 1 < ROUNDS:
+                normalise(r - 1)
+            if step == 0 and 0 <= r - 2 < ROUNDS:
+                regroup_sampled(r - 2)
+            if step == 1 and 0 <= r - 2 < ROUNDS:
+                quantise_sampled(r - 2)
+            if step == 3 and 0 <= r - 2 < ROUNDS:
+                store(r - 2)
+            if top is not None:
+                row_shift(n - 1, top)

@@ -49,9 +49,10 @@ def tile_attentionalsplatting_pb_kernel(
         keep = stack.enter_context(tc.tile_pool(name="keep", bufs=1))
         values = stack.enter_context(tc.tile_pool(name="values", bufs=1))
         stats = stack.enter_context(tc.tile_pool(name="stats", bufs=6))
-        psum_s = stack.enter_context(tc.psum_pool(name="psum_s", bufs=4))
+        psum_s = stack.enter_context(tc.psum_pool(name="psum_s", bufs=3))
         psum_t = stack.enter_context(tc.psum_pool(name="psum_t", bufs=2))
-        psum_m = stack.enter_context(tc.psum_pool(name="psum_m", bufs=2))
+        psum_v = stack.enter_context(tc.psum_pool(name="psum_v", bufs=1))
+        psum_o = stack.enter_context(tc.psum_pool(name="psum_o", bufs=2))
 
         trk_j = const.tile([P, T * JB, 2], BF16)
         trk_v = const.tile([P, T, SLOTS, 2], BF16)
@@ -257,7 +258,8 @@ def tile_attentionalsplatting_pb_kernel(
 
         work = stack.enter_context(tc.tile_pool(name="work", bufs=2))
         sc_of, shift_of, e_of, et_of, eg_of = {}, {}, {}, {}, {}
-        rowsum_of, codes_of, scales_of, pv_of, sampled_of, st_of, sg_of, po_of = {}, {}, {}, {}, {}, {}, {}, {}
+        rowsum_of, e_codes_of, e_scales_of, pv_of, sampled_of, st_of, sg_of = {}, {}, {}, {}, {}, {}, {}
+        s_codes_of, s_scales_of, po_of, o_of = {}, {}, {}, {}
 
         def copy_q(r, qt_ps):
             q_t[r] = work.tile([P, H, P], BF16, tag="q_t", name="q_t")
@@ -288,9 +290,8 @@ def tile_attentionalsplatting_pb_kernel(
             nc.vector.tensor_scalar_mul(out=shift_of[n][:], in0=top[:], scalar1=-SCALE)
 
         def exponent(n):
-            r, h = divmod(n, H)
-            if h == 0:
-                rowsum_of[r] = stats.tile([P, H], F32, tag="rowsum", name="rowsum")
+            if n % 4 == 0:
+                rowsum_of[n // 4] = stats.tile([P, 4], F32, tag="rowsum", name="rowsum")
             if n % 2 == 0:
                 e_of[n // 2] = work.tile([P, 2, M], BF16, tag="e_sb", name="e_sb", bufs=3)
             nc.scalar.activation(
@@ -299,7 +300,7 @@ def tile_attentionalsplatting_pb_kernel(
                 func=ACT.Exp,
                 bias=shift_of[n][:],
                 scale=SCALE,
-                accum_out=rowsum_of[r][:, h : h + 1],
+                accum_out=rowsum_of[n // 4][:, n % 4 : n % 4 + 1],
             )
 
         def transpose_e(m):
@@ -320,13 +321,11 @@ def tile_attentionalsplatting_pb_kernel(
                 nc.scalar.copy(out=eg_of[m][:], in_=et_of[m][:].rearrange("p h u i -> p h i u"))
 
         def quantise_e(m):
-            r, hp = divmod(m, H // 2)
-            if hp == 0:
-                codes_of[r] = work.tile([P, H * P], U32, tag="e_codes", name="e_codes", align_bytes=64)
-                scales_of[r] = work.tile([P, H * P], U8, tag="e_scales", name="e_scales", align_bytes=64)
+            e_codes_of[m] = work.tile([P, 2 * P], U32, tag="e_codes", name="e_codes", bufs=3, align_bytes=64)
+            e_scales_of[m] = work.tile([P, 2 * P], U8, tag="e_scales", name="e_scales", bufs=3, align_bytes=64)
             nc.vector.quantize_mx(
-                out=codes_of[r][:, cols(hp, 2 * P)].bitcast(FP8X4),
-                scales=scales_of[r][:, cols(hp, 2 * P)],
+                out=e_codes_of[m][:].bitcast(FP8X4),
+                scales=e_scales_of[m][:],
                 in_=eg_of[m][:].rearrange("p h i u -> p (h i u)").bitcast(BF16),
             )
 
@@ -338,114 +337,112 @@ def tile_attentionalsplatting_pb_kernel(
                     in_=v_grouped[t, half][:].rearrange("p i w s -> p (i w s)"),
                 )
 
-        def multiply_values(r):
-            t = r // IT
-            for half in range(2):
-                pv_of[r, half] = psum_m.tile([P, 4, DH], F32, tag="mm", name="pv")
-                for hq in range(4):
-                    h = 4 * half + hq
-                    nc.tensor.matmul_mx(
-                        out=pv_of[r, half][:, hq, :],
-                        lhsT=codes_of[r][:, cols(h, P)].bitcast(FP8X4),
-                        lhsT_scale=scales_of[r][:, cols(h, P)],
-                        rhs=v_codes[t][:, cols(h, DH)].bitcast(FP8X4),
-                        rhs_scale=v_scales[t][:, cols(h, DH)],
-                        start=True,
-                        stop=True,
-                    )
-
-        def normalise(r):
-            inv_sum = stats.tile([P, H], F32, tag="inv_sum")
-            nc.vector.reciprocal(out=inv_sum[:], in_=rowsum_of[r][:])
-            sampled_of[r] = work.tile([P, 2, 4, DH], BF16, tag="sampled", name="sampled")
-            for half in range(2):
-                nc.vector.tensor_tensor(
-                    out=sampled_of[r][:, half, :, :],
-                    in0=pv_of[r, half][:],
-                    in1=inv_sum[:, cols(half, 4)].unsqueeze(2).to_broadcast([P, 4, DH]),
-                    op=ALU.mult,
+        def multiply_values(m):
+            k = m // 2
+            t = m // (IT * H // 2)
+            if m % 2 == 0:
+                pv_of[k] = psum_v.tile([P, 4, DH], F32, tag="pv", name="pv")
+            for hh in range(2):
+                h = (2 * m + hh) % H
+                nc.tensor.matmul_mx(
+                    out=pv_of[k][:, h % 4, :],
+                    lhsT=e_codes_of[m][:, cols(hh, P)].bitcast(FP8X4),
+                    lhsT_scale=e_scales_of[m][:, cols(hh, P)],
+                    rhs=v_codes[t][:, cols(h, DH)].bitcast(FP8X4),
+                    rhs_scale=v_scales[t][:, cols(h, DH)],
+                    start=True,
+                    stop=True,
                 )
 
-        def transpose_sampled(r):
-            st_of[r] = psum_t.tile([P, 2, 2, P], F32, tag="tp", name="st_ps")
-            words = sampled_of[r][:].rearrange("p a b c -> p (a b c)").bitcast(F32)
-            for g in range(2):
-                for u in range(2):
-                    nc.tensor.transpose(out=st_of[r][:, g, u, :], in_=words[:, cols(2 * g + u, P)], identity=ident_f[:])
-
-        def regroup_sampled(r):
-            sg_of[r] = work.tile([P, 2, P, 2], F32, tag="s_grouped", name="s_grouped", align_bytes=64)
-            nc.scalar.copy(out=sg_of[r][:], in_=st_of[r][:].rearrange("p g u i -> p g i u"))
-
-        def quantise_sampled(r):
-            s_codes = work.tile([P, 2 * P], U32, tag="s_codes", align_bytes=64)
-            s_scales = work.tile([P, 2 * P], U8, tag="s_scales", align_bytes=64)
-            nc.vector.quantize_mx(
-                out=s_codes[:].bitcast(FP8X4),
-                scales=s_scales[:],
-                in_=sg_of[r][:].rearrange("p g i u -> p (g i u)").bitcast(BF16),
+        def normalise(k):
+            inv_sum = stats.tile([P, 4], F32, tag="inv_sum")
+            nc.vector.reciprocal(out=inv_sum[:], in_=rowsum_of[k][:])
+            sampled_of[k] = work.tile([P, 4, DH], BF16, tag="sampled", name="sampled")
+            nc.vector.tensor_tensor(
+                out=sampled_of[k][:],
+                in0=pv_of[k][:],
+                in1=inv_sum[:].unsqueeze(2).to_broadcast([P, 4, DH]),
+                op=ALU.mult,
             )
-            sg_of[r] = (s_codes, s_scales)
 
-        def project(r):
-            s_codes, s_scales = sg_of[r]
-            for nh in range(2):
-                po_of[r, nh] = psum_m.tile([P, 512], F32, tag="mm", name="po")
-                for g in range(2):
-                    nc.tensor.matmul_mx(
-                        out=po_of[r, nh][:],
-                        lhsT=s_codes[:, cols(g, P)].bitcast(FP8X4),
-                        lhsT_scale=s_scales[:, cols(g, P)],
-                        rhs=w_codes[:, g, cols(nh, 512)].bitcast(FP8X4),
-                        rhs_scale=w_scales[:, g, cols(nh, 512)],
-                        start=(g == 0),
-                        stop=(g == 1),
-                    )
+        def transpose_sampled(k):
+            st_of[k] = psum_t.tile([P, 2, P], F32, tag="tp", name="st_ps")
+            words = sampled_of[k][:].rearrange("p b c -> p (b c)").bitcast(F32)
+            for u in range(2):
+                nc.tensor.transpose(out=st_of[k][:, u, :], in_=words[:, cols(u, P)], identity=ident_f[:])
 
-        def store(r):
+        def regroup_sampled(k):
+            sg_of[k] = work.tile([P, P, 2], F32, tag="s_grouped", name="s_grouped", align_bytes=64)
+            nc.scalar.copy(out=sg_of[k][:], in_=st_of[k][:].rearrange("p u i -> p i u"))
+
+        def quantise_sampled(k):
+            s_codes_of[k] = work.tile([P, P], U32, tag="s_codes", name="s_codes", bufs=3, align_bytes=64)
+            s_scales_of[k] = work.tile([P, P], U8, tag="s_scales", name="s_scales", bufs=3, align_bytes=64)
+            nc.vector.quantize_mx(
+                out=s_codes_of[k][:].bitcast(FP8X4),
+                scales=s_scales_of[k][:],
+                in_=sg_of[k][:].rearrange("p i u -> p (i u)").bitcast(BF16),
+            )
+
+        def project(k, nh):
+            r, g = divmod(k, 2)
+            if g == 0:
+                po_of[r, nh] = psum_o.tile([P, 512], F32, tag="po", name="po")
+            nc.tensor.matmul_mx(
+                out=po_of[r, nh][:],
+                lhsT=s_codes_of[k][:].bitcast(FP8X4),
+                lhsT_scale=s_scales_of[k][:],
+                rhs=w_codes[:, g, cols(nh, 512)].bitcast(FP8X4),
+                rhs_scale=w_scales[:, g, cols(nh, 512)],
+                start=(g == 0),
+                stop=(g == 1),
+            )
+
+        def store(r, nh):
             t, it = divmod(r, IT)
-            o_sb = work.tile([P, D], F32, tag="o_sb")
-            for nh in range(2):
-                nc.scalar.copy(out=o_sb[:, cols(nh, 512)], in_=po_of[r, nh][:])
-            nc.sync.dma_start(out=out[t, cols(it, P), :], in_=o_sb[:])
+            if nh == 0:
+                o_of[r] = work.tile([P, D], F32, tag="o_sb", name="o_sb")
+            nc.scalar.copy(out=o_of[r][:, cols(nh, 512)], in_=po_of[r, nh][:])
+            if nh == 1:
+                nc.sync.dma_start(out=out[t, cols(it, P), :], in_=o_of[r][:])
 
         heads = ROUNDS * H
         copy_q(0, transpose_q(0))
         load_q(4)
         next_q = {}
-        for n in range(heads + 20):
-            if n >= 4 and n % 2 == 0 and (n - 4) // 2 < heads // 2:
-                transpose_e((n - 4) // 2)
+        for n in range(heads + 16):
             r, step = divmod(n, H)
+            if n % 2 == 0 and 0 <= (n - 4) // 2 < heads // 2:
+                transpose_e((n - 4) // 2)
+            if (n - 11) % 4 == 0 and 0 <= (n - 11) // 4 < heads // 4:
+                transpose_sampled((n - 11) // 4)
             if step == 5 and r + 1 < ROUNDS:
                 next_q[r + 1] = transpose_q(r + 1)
                 load_q(r + 5)
-            if step == 7 and 0 <= r - 1 < ROUNDS:
-                transpose_sampled(r - 1)
             if n < heads:
                 scores(n)
-            if step == 5 and 0 <= r - 1 < ROUNDS:
-                multiply_values(r - 1)
-            if step == 2 and 0 <= r - 2 < ROUNDS:
-                project(r - 2)
+            if n % 2 == 1 and 0 <= (n - 7) // 2 < heads // 2:
+                multiply_values((n - 7) // 2)
+            if n % 2 == 1 and 0 <= (n - 15) // 4 < heads // 4:
+                project((n - 15) // 4, ((n - 15) % 4) // 2)
             top = row_max(n - 1) if 0 <= n - 1 < heads else None
             if 0 <= n - 2 < heads:
                 exponent(n - 2)
-            if n >= 5 and n % 2 == 1 and (n - 5) // 2 < heads // 2:
+            if n % 2 == 1 and 0 <= (n - 5) // 2 < heads // 2:
                 regroup_e((n - 5) // 2)
-            if n >= 6 and n % 2 == 0 and (n - 6) // 2 < heads // 2:
+            if n % 2 == 0 and 0 <= (n - 6) // 2 < heads // 2:
                 quantise_e((n - 6) // 2)
-            if step == 3 and 0 <= r - 1 < ROUNDS and (r - 1) % IT == 0:
-                quantise_values((r - 1) // IT)
+            if (n - 5) % (IT * H) == 0 and (n - 5) // (IT * H) < T:
+                quantise_values((n - 5) // (IT * H))
             if step == 6 and r + 1 < ROUNDS:
                 copy_q(r + 1, next_q[r + 1])
-            if step == 6 and 0 <= r - 1 < ROUNDS:
-                normalise(r - 1)
-            if step == 0 and 0 <= r - 2 < ROUNDS:
-                regroup_sampled(r - 2)
-            if step == 1 and 0 <= r - 2 < ROUNDS:
-                quantise_sampled(r - 2)
-            if step == 3 and 0 <= r - 2 < ROUNDS:
-                store(r - 2)
+            if (n - 10) % 4 == 0 and 0 <= (n - 10) // 4 < heads // 4:
+                normalise((n - 10) // 4)
+            if (n - 12) % 4 == 0 and 0 <= (n - 12) // 4 < heads // 4:
+                regroup_sampled((n - 12) // 4)
+            if (n - 13) % 4 == 0 and 0 <= (n - 13) // 4 < heads // 4:
+                quantise_sampled((n - 13) // 4)
+            if n % 2 == 0 and 0 <= (n - 20) // 8 < ROUNDS and (n - 20) % 8 < 4:
+                store((n - 20) // 8, ((n - 20) % 8) // 2)
             if top is not None:
                 row_shift(n - 1, top)

@@ -45,14 +45,13 @@ def tile_attentionalsplatting_pb_kernel(
     with ExitStack() as stack:
         stack.enter_context(tc.manual_schedule())
         const = stack.enter_context(tc.tile_pool(name="const", bufs=1))
-        q_pool = stack.enter_context(tc.tile_pool(name="q_pool", bufs=4))
+        q_pool = stack.enter_context(tc.tile_pool(name="q_pool", bufs=3))
         keep = stack.enter_context(tc.tile_pool(name="keep", bufs=1))
         values = stack.enter_context(tc.tile_pool(name="values", bufs=1))
         stats = stack.enter_context(tc.tile_pool(name="stats", bufs=6))
-        psum_s = stack.enter_context(tc.psum_pool(name="psum_s", bufs=3))
+        psum_s = stack.enter_context(tc.psum_pool(name="psum_s", bufs=4))
         psum_t = stack.enter_context(tc.psum_pool(name="psum_t", bufs=2))
-        psum_v = stack.enter_context(tc.psum_pool(name="psum_v", bufs=1))
-        psum_o = stack.enter_context(tc.psum_pool(name="psum_o", bufs=2))
+        psum_m = stack.enter_context(tc.psum_pool(name="psum_m", bufs=2))
 
         trk_j = const.tile([P, T * JB, 2], BF16)
         trk_v = const.tile([P, T, SLOTS, 2], BF16)
@@ -115,7 +114,6 @@ def tile_attentionalsplatting_pb_kernel(
             load_tok(1)
             load_q(1)
             load_q(2)
-            load_q(3)
 
             make_identity(nc, ident_bf[:])
             make_identity(nc, ident_f[:])
@@ -154,6 +152,23 @@ def tile_attentionalsplatting_pb_kernel(
                 dx2, dy2 = squares[t, jb, 0], squares[t, jb, 1]
                 nc.vector.tensor_tensor(out=dx2[:], in0=dx2[:], in1=dy2[:], op=ALU.add)
                 nc.vector.tensor_scalar_mul(out=bias_t[t][:, jb, :], in0=dx2[:], scalar1=-BIAS_GAIN)
+
+            def bias_on_gpsimd(t, jb):
+                apart = [values.tile([P, HW], F32, tag="apart%d" % c, name="apart%d" % c) for c in range(2)]
+                for c in range(2):
+                    nc.gpsimd.tensor_scalar(
+                        out=apart[c][:],
+                        in0=fxy[:, c, :],
+                        scalar1=1.0,
+                        scalar2=neg_trk[:, t * JB + jb, c : c + 1],
+                        op0=ALU.mult,
+                        op1=ALU.add,
+                    )
+                    nc.gpsimd.tensor_tensor(out=apart[c][:], in0=apart[c][:], in1=apart[c][:], op=ALU.mult)
+                nc.gpsimd.tensor_tensor(out=apart[0][:], in0=apart[0][:], in1=apart[1][:], op=ALU.add)
+                nc.gpsimd.tensor_scalar(
+                    out=bias_t[t][:, jb, :], in0=apart[0][:], scalar1=-BIAS_GAIN, scalar2=0.0, op0=ALU.mult, op1=ALU.add
+                )
 
             def transpose_keys(t, hp):
                 kt_ps = psum_t.tile([P, 2, JB, P], BF16, tag="tp", name="kt_ps")
@@ -236,30 +251,34 @@ def tile_attentionalsplatting_pb_kernel(
                     in_=w_grouped[:].rearrange("p o u -> p (o u)").bitcast(BF16),
                 )
 
-            for t in range(T):
-                square_distances(t, 0)
-                square_distances(t, 1)
-                angle_tables(t, 0)
-                rotate_values(t, 0)
-                finish_bias(t, 0)
-                finish_bias(t, 1)
-                square_distances(t, 2)
-                square_distances(t, 3)
-                angle_tables(t, 1)
-                rotate_values(t, 1)
-                finish_bias(t, 2)
-                finish_bias(t, 3)
-                for hp in range(H // 2):
-                    transpose_keys(t, hp)
-                if t + 1 < T:
-                    load_k(t + 1)
+            square_distances(0, 0)
+            square_distances(0, 1)
+            angle_tables(0, 0)
+            rotate_values(0, 0)
+            finish_bias(0, 0)
+            finish_bias(0, 1)
+            square_distances(0, 2)
+            square_distances(0, 3)
+            angle_tables(0, 1)
+            rotate_values(0, 1)
+            finish_bias(0, 2)
+            finish_bias(0, 3)
+            for hp in range(H // 2):
+                transpose_keys(0, hp)
+            load_k(1)
+            for jb in range(JB):
+                bias_on_gpsimd(1, jb)
+            for half in range(2):
+                angle_tables(1, half)
+                rotate_values(1, half)
+            for hp in range(H // 2):
+                transpose_keys(1, hp)
             for g in range(2):
                 quantise_weights(g)
 
         work = stack.enter_context(tc.tile_pool(name="work", bufs=2))
         sc_of, shift_of, e_of, et_of, eg_of = {}, {}, {}, {}, {}
-        rowsum_of, e_codes_of, e_scales_of, pv_of, sampled_of, st_of, sg_of = {}, {}, {}, {}, {}, {}, {}
-        s_codes_of, s_scales_of, po_of, o_of = {}, {}, {}, {}
+        rowsum_of, codes_of, scales_of, pv_of, sampled_of, st_of, sg_of, po_of = {}, {}, {}, {}, {}, {}, {}, {}
 
         def copy_q(r, qt_ps):
             q_t[r] = work.tile([P, H, P], BF16, tag="q_t", name="q_t")
@@ -280,27 +299,32 @@ def tile_attentionalsplatting_pb_kernel(
                 )
             nc.tensor.matmul(out=sc_of[n][:], lhsT=q_t[r][:, h, :], rhs=k_t[t][:, h, :], start=False, stop=True)
 
-        def row_max(n):
-            top = stats.tile([P, 1], F32, tag="top")
-            nc.vector.tensor_reduce(out=top[:], in_=sc_of[n][:], axis=AX.X, op=ALU.max)
-            return top
-
-        def row_shift(n, top):
+        def row_shift(n):
             shift_of[n] = stats.tile([P, 1], F32, tag="shift", name="shift")
-            nc.vector.tensor_scalar_mul(out=shift_of[n][:], in0=top[:], scalar1=-SCALE)
+            unread = work.tile([P, M], BF16, tag="unread")
+            nc.vector.tensor_scalar(
+                out=unread[:],
+                in0=sc_of[n][:],
+                scalar1=-SCALE,
+                scalar2=None,
+                op0=ALU.mult,
+                op1=ALU.min,
+                accum_out=shift_of[n][:],
+            )
 
         def exponent(n):
-            if n % 4 == 0:
-                rowsum_of[n // 4] = stats.tile([P, 4], F32, tag="rowsum", name="rowsum")
+            r, h = divmod(n, H)
+            if h == 0:
+                rowsum_of[r] = stats.tile([P, H], F32, tag="rowsum", name="rowsum")
             if n % 2 == 0:
-                e_of[n // 2] = work.tile([P, 2, M], BF16, tag="e_sb", name="e_sb", bufs=3)
+                e_of[n // 2] = work.tile([P, 2, M], BF16, tag="e_sb", name="e_sb", bufs=4)
             nc.scalar.activation(
                 out=e_of[n // 2][:, n % 2, :],
                 in_=sc_of[n][:],
                 func=ACT.Exp,
                 bias=shift_of[n][:],
                 scale=SCALE,
-                accum_out=rowsum_of[n // 4][:, n % 4 : n % 4 + 1],
+                accum_out=rowsum_of[r][:, h : h + 1],
             )
 
         def transpose_e(m):
@@ -315,17 +339,16 @@ def tile_attentionalsplatting_pb_kernel(
 
         def regroup_e(m):
             eg_of[m] = work.tile([P, 2, P, 2], F32, tag="e_grouped", name="e_grouped", bufs=3, align_bytes=64)
-            if m % 2 == 0:
-                nc.vector.tensor_copy(out=eg_of[m][:], in_=et_of[m][:].rearrange("p h u i -> p h i u"))
-            else:
-                nc.scalar.copy(out=eg_of[m][:], in_=et_of[m][:].rearrange("p h u i -> p h i u"))
+            nc.scalar.copy(out=eg_of[m][:], in_=et_of[m][:].rearrange("p h u i -> p h i u"))
 
         def quantise_e(m):
-            e_codes_of[m] = work.tile([P, 2 * P], U32, tag="e_codes", name="e_codes", bufs=3, align_bytes=64)
-            e_scales_of[m] = work.tile([P, 2 * P], U8, tag="e_scales", name="e_scales", bufs=3, align_bytes=64)
+            r, hp = divmod(m, H // 2)
+            if hp == 0:
+                codes_of[r] = work.tile([P, H * P], U32, tag="e_codes", name="e_codes", align_bytes=64)
+                scales_of[r] = work.tile([P, H * P], U8, tag="e_scales", name="e_scales", align_bytes=64)
             nc.vector.quantize_mx(
-                out=e_codes_of[m][:].bitcast(FP8X4),
-                scales=e_scales_of[m][:],
+                out=codes_of[r][:, cols(hp, 2 * P)].bitcast(FP8X4),
+                scales=scales_of[r][:, cols(hp, 2 * P)],
                 in_=eg_of[m][:].rearrange("p h i u -> p (h i u)").bitcast(BF16),
             )
 
@@ -337,112 +360,113 @@ def tile_attentionalsplatting_pb_kernel(
                     in_=v_grouped[t, half][:].rearrange("p i w s -> p (i w s)"),
                 )
 
-        def multiply_values(m):
-            k = m // 2
-            t = m // (IT * H // 2)
-            if m % 2 == 0:
-                pv_of[k] = psum_v.tile([P, 4, DH], F32, tag="pv", name="pv")
-            for hh in range(2):
-                h = (2 * m + hh) % H
-                nc.tensor.matmul_mx(
-                    out=pv_of[k][:, h % 4, :],
-                    lhsT=e_codes_of[m][:, cols(hh, P)].bitcast(FP8X4),
-                    lhsT_scale=e_scales_of[m][:, cols(hh, P)],
-                    rhs=v_codes[t][:, cols(h, DH)].bitcast(FP8X4),
-                    rhs_scale=v_scales[t][:, cols(h, DH)],
-                    start=True,
-                    stop=True,
+        def multiply_values(r):
+            t = r // IT
+            for half in range(2):
+                pv_of[r, half] = psum_m.tile([P, 4, DH], F32, tag="mm", name="pv")
+                for hq in range(4):
+                    h = 4 * half + hq
+                    nc.tensor.matmul_mx(
+                        out=pv_of[r, half][:, hq, :],
+                        lhsT=codes_of[r][:, cols(h, P)].bitcast(FP8X4),
+                        lhsT_scale=scales_of[r][:, cols(h, P)],
+                        rhs=v_codes[t][:, cols(h, DH)].bitcast(FP8X4),
+                        rhs_scale=v_scales[t][:, cols(h, DH)],
+                        start=True,
+                        stop=True,
+                    )
+
+        def normalise(r):
+            inv_sum = stats.tile([P, H], F32, tag="inv_sum")
+            nc.vector.reciprocal(out=inv_sum[:], in_=rowsum_of[r][:])
+            sampled_of[r] = work.tile([P, 2, 4, DH], BF16, tag="sampled", name="sampled")
+            for half in range(2):
+                nc.vector.tensor_tensor(
+                    out=sampled_of[r][:, half, :, :],
+                    in0=pv_of[r, half][:],
+                    in1=inv_sum[:, cols(half, 4)].unsqueeze(2).to_broadcast([P, 4, DH]),
+                    op=ALU.mult,
                 )
 
-        def normalise(k):
-            inv_sum = stats.tile([P, 4], F32, tag="inv_sum")
-            nc.vector.reciprocal(out=inv_sum[:], in_=rowsum_of[k][:])
-            sampled_of[k] = work.tile([P, 4, DH], BF16, tag="sampled", name="sampled")
-            nc.vector.tensor_tensor(
-                out=sampled_of[k][:],
-                in0=pv_of[k][:],
-                in1=inv_sum[:].unsqueeze(2).to_broadcast([P, 4, DH]),
-                op=ALU.mult,
-            )
+        def transpose_sampled(r):
+            st_of[r] = psum_t.tile([P, 2, 2, P], F32, tag="tp", name="st_ps")
+            words = sampled_of[r][:].rearrange("p a b c -> p (a b c)").bitcast(F32)
+            for g in range(2):
+                for u in range(2):
+                    nc.tensor.transpose(out=st_of[r][:, g, u, :], in_=words[:, cols(2 * g + u, P)], identity=ident_f[:])
 
-        def transpose_sampled(k):
-            st_of[k] = psum_t.tile([P, 2, P], F32, tag="tp", name="st_ps")
-            words = sampled_of[k][:].rearrange("p b c -> p (b c)").bitcast(F32)
-            for u in range(2):
-                nc.tensor.transpose(out=st_of[k][:, u, :], in_=words[:, cols(u, P)], identity=ident_f[:])
+        def regroup_sampled(r):
+            sg_of[r] = work.tile([P, 2, P, 2], F32, tag="s_grouped", name="s_grouped", align_bytes=64)
+            nc.scalar.copy(out=sg_of[r][:], in_=st_of[r][:].rearrange("p g u i -> p g i u"))
 
-        def regroup_sampled(k):
-            sg_of[k] = work.tile([P, P, 2], F32, tag="s_grouped", name="s_grouped", align_bytes=64)
-            nc.scalar.copy(out=sg_of[k][:], in_=st_of[k][:].rearrange("p u i -> p i u"))
-
-        def quantise_sampled(k):
-            s_codes_of[k] = work.tile([P, P], U32, tag="s_codes", name="s_codes", bufs=3, align_bytes=64)
-            s_scales_of[k] = work.tile([P, P], U8, tag="s_scales", name="s_scales", bufs=3, align_bytes=64)
+        def quantise_sampled(r):
+            s_codes = work.tile([P, 2 * P], U32, tag="s_codes", align_bytes=64)
+            s_scales = work.tile([P, 2 * P], U8, tag="s_scales", align_bytes=64)
             nc.vector.quantize_mx(
-                out=s_codes_of[k][:].bitcast(FP8X4),
-                scales=s_scales_of[k][:],
-                in_=sg_of[k][:].rearrange("p i u -> p (i u)").bitcast(BF16),
+                out=s_codes[:].bitcast(FP8X4),
+                scales=s_scales[:],
+                in_=sg_of[r][:].rearrange("p g i u -> p (g i u)").bitcast(BF16),
             )
+            sg_of[r] = (s_codes, s_scales)
 
-        def project(k, nh):
-            r, g = divmod(k, 2)
-            if g == 0:
-                po_of[r, nh] = psum_o.tile([P, 512], F32, tag="po", name="po")
-            nc.tensor.matmul_mx(
-                out=po_of[r, nh][:],
-                lhsT=s_codes_of[k][:].bitcast(FP8X4),
-                lhsT_scale=s_scales_of[k][:],
-                rhs=w_codes[:, g, cols(nh, 512)].bitcast(FP8X4),
-                rhs_scale=w_scales[:, g, cols(nh, 512)],
-                start=(g == 0),
-                stop=(g == 1),
-            )
+        def project(r):
+            s_codes, s_scales = sg_of[r]
+            for nh in range(2):
+                po_of[r, nh] = psum_m.tile([P, 512], F32, tag="mm", name="po")
+                for g in range(2):
+                    nc.tensor.matmul_mx(
+                        out=po_of[r, nh][:],
+                        lhsT=s_codes[:, cols(g, P)].bitcast(FP8X4),
+                        lhsT_scale=s_scales[:, cols(g, P)],
+                        rhs=w_codes[:, g, cols(nh, 512)].bitcast(FP8X4),
+                        rhs_scale=w_scales[:, g, cols(nh, 512)],
+                        start=(g == 0),
+                        stop=(g == 1),
+                    )
 
-        def store(r, nh):
+        def store(r):
             t, it = divmod(r, IT)
-            if nh == 0:
-                o_of[r] = work.tile([P, D], F32, tag="o_sb", name="o_sb")
-            nc.scalar.copy(out=o_of[r][:, cols(nh, 512)], in_=po_of[r, nh][:])
-            if nh == 1:
-                nc.sync.dma_start(out=out[t, cols(it, P), :], in_=o_of[r][:])
+            o_sb = work.tile([P, D], F32, tag="o_sb")
+            for nh in range(2):
+                nc.scalar.copy(out=o_sb[:, cols(nh, 512)], in_=po_of[r, nh][:])
+            nc.sync.dma_start(out=out[t, cols(it, P), :], in_=o_sb[:])
 
         heads = ROUNDS * H
         copy_q(0, transpose_q(0))
-        load_q(4)
+        load_q(3)
         next_q = {}
-        for n in range(heads + 16):
+        for n in range(heads + 24):
             r, step = divmod(n, H)
-            if n % 2 == 0 and 0 <= (n - 4) // 2 < heads // 2:
-                transpose_e((n - 4) // 2)
-            if (n - 11) % 4 == 0 and 0 <= (n - 11) // 4 < heads // 4:
-                transpose_sampled((n - 11) // 4)
+            if step == 2 and 0 <= r - 2 < ROUNDS:
+                transpose_sampled(r - 2)
+            if n % 2 == 0 and 0 <= (n - 6) // 2 < heads // 2:
+                transpose_e((n - 6) // 2)
             if step == 5 and r + 1 < ROUNDS:
                 next_q[r + 1] = transpose_q(r + 1)
-                load_q(r + 5)
+                load_q(r + 4)
             if n < heads:
                 scores(n)
-            if n % 2 == 1 and 0 <= (n - 7) // 2 < heads // 2:
-                multiply_values((n - 7) // 2)
-            if n % 2 == 1 and 0 <= (n - 15) // 4 < heads // 4:
-                project((n - 15) // 4, ((n - 15) % 4) // 2)
-            top = row_max(n - 1) if 0 <= n - 1 < heads else None
+            if step == 7 and 0 <= r - 1 < ROUNDS:
+                multiply_values(r - 1)
+            if step == 5 and 0 <= r - 2 < ROUNDS:
+                project(r - 2)
+            if 0 <= n - 1 < heads:
+                row_shift(n - 1)
             if 0 <= n - 2 < heads:
                 exponent(n - 2)
-            if n % 2 == 1 and 0 <= (n - 5) // 2 < heads // 2:
-                regroup_e((n - 5) // 2)
-            if n % 2 == 0 and 0 <= (n - 6) // 2 < heads // 2:
-                quantise_e((n - 6) // 2)
-            if (n - 5) % (IT * H) == 0 and (n - 5) // (IT * H) < T:
-                quantise_values((n - 5) // (IT * H))
+            if n % 2 == 1 and 0 <= (n - 7) // 2 < heads // 2:
+                regroup_e((n - 7) // 2)
+            if n % 2 == 0 and 0 <= (n - 8) // 2 < heads // 2:
+                quantise_e((n - 8) // 2)
             if step == 6 and r + 1 < ROUNDS:
                 copy_q(r + 1, next_q[r + 1])
-            if (n - 10) % 4 == 0 and 0 <= (n - 10) // 4 < heads // 4:
-                normalise((n - 10) // 4)
-            if (n - 12) % 4 == 0 and 0 <= (n - 12) // 4 < heads // 4:
-                regroup_sampled((n - 12) // 4)
-            if (n - 13) % 4 == 0 and 0 <= (n - 13) // 4 < heads // 4:
-                quantise_sampled((n - 13) // 4)
-            if n % 2 == 0 and 0 <= (n - 20) // 8 < ROUNDS and (n - 20) % 8 < 4:
-                store((n - 20) // 8, ((n - 20) % 8) // 2)
-            if top is not None:
-                row_shift(n - 1, top)
+            if step == 5 and 0 <= r - 1 < ROUNDS and (r - 1) % IT == 0:
+                quantise_values((r - 1) // IT)
+            if step == 0 and 0 <= r - 2 < ROUNDS:
+                normalise(r - 2)
+            if step == 3 and 0 <= r - 2 < ROUNDS:
+                regroup_sampled(r - 2)
+            if step == 4 and 0 <= r - 2 < ROUNDS:
+                quantise_sampled(r - 2)
+            if step == 6 and 0 <= r - 2 < ROUNDS:
+                store(r - 2)

@@ -6,12 +6,12 @@ from concourse.masks import make_identity
 
 F32 = mybir.dt.float32
 BF16 = mybir.dt.bfloat16
+I32 = mybir.dt.int32
 U32 = mybir.dt.uint32
 U8 = mybir.dt.uint8
 FP8X4 = mybir.dt.float8_e4m3fn_x4
 ALU = mybir.AluOpType
 ACT = mybir.ActivationFunctionType
-AX = mybir.AxisListType
 
 P = 128
 T = 2
@@ -23,13 +23,18 @@ DH = D // H
 IT = HW // P
 JB = M // P
 ROUNDS = T * IT
-PAIRS = 256
+DUOS = H // 2
+STEPS = ROUNDS * DUOS
+THETAS = 256
 SLOTS = 4
+CHUNK = 256
+CHUNKS = T * HW // CHUNK
+PIECE = 64
 
 SCALE = 1.0 / math.sqrt(DH)
 BIAS_GAIN = 2.0 / SCALE
 TURN = 2.0 * math.pi
-ROUND_MAGIC = 12582912.0
+VALUES_STEP = 12
 
 FLOPS = 2 * (2 * T * H * HW * M * DH) + 2 * T * HW * D * D
 
@@ -44,287 +49,304 @@ def tile_attentionalsplatting_pb_kernel(
     nc = tc.nc
     with ExitStack() as stack:
         stack.enter_context(tc.manual_schedule())
-        const = stack.enter_context(tc.tile_pool(name="const", bufs=1))
-        q_pool = stack.enter_context(tc.tile_pool(name="q_pool", bufs=3))
         keep = stack.enter_context(tc.tile_pool(name="keep", bufs=1))
-        values = stack.enter_context(tc.tile_pool(name="values", bufs=1))
-        stats = stack.enter_context(tc.tile_pool(name="stats", bufs=6))
+        work = stack.enter_context(tc.tile_pool(name="work", bufs=2))
         psum_s = stack.enter_context(tc.psum_pool(name="psum_s", bufs=4))
         psum_t = stack.enter_context(tc.psum_pool(name="psum_t", bufs=2))
         psum_m = stack.enter_context(tc.psum_pool(name="psum_m", bufs=2))
 
-        trk_j = const.tile([P, T * JB, 2], BF16)
-        trk_v = const.tile([P, T, SLOTS, 2], BF16)
-        fpos = const.tile([P, 2 * HW], BF16)
+        trk_j = keep.tile([P, T * JB, 2], BF16)
+        trk_v = keep.tile([P, T, SLOTS, 2], BF16)
+        fpos = keep.tile([P, IT, 2], BF16)
         with nc.allow_non_contiguous_dma(reason="a few KiB of positions"):
-            nc.scalar.dma_start(out=trk_j[:], in_=tracks.rearrange("t (jb p) c -> p (t jb) c", p=P))
             nc.scalar.dma_start(
                 out=trk_v[:].rearrange("p t (u e) c -> p (t u) (e c)", u=2),
                 in_=tracks.rearrange("t (u p e) c -> p (t u) (e c)", u=2, p=P),
             )
-            nc.scalar.dma_start(
-                out=fpos[:], in_=feature_positions.rearrange("i c -> (i c)").partition_broadcast(P)
-            )
+            nc.scalar.dma_start(out=trk_j[:], in_=tracks.rearrange("t (jb p) c -> p (t jb) c", p=P))
+            nc.scalar.dma_start(out=fpos[:], in_=feature_positions.rearrange("(it p) c -> p it c", p=P))
 
-        q_tiles = {}
+        q_sb, k_sb, tok, q_t = {}, {}, {}, {}
 
         def load_q(r):
             if r < ROUNDS:
-                q_tiles[r] = q_pool.tile([P, D], BF16, tag="q_sb", name="q_sb%d" % r)
-                nc.sync.dma_start(out=q_tiles[r][:], in_=q_norm[r // IT, cols(r % IT, P), :])
+                q_sb[r] = work.tile([P, D], BF16, tag="q_sb", name="q_sb", bufs=3)
+                nc.sync.dma_start(out=q_sb[r][:], in_=q_norm[r // IT, cols(r % IT, P), :])
 
-        tok = [values.tile([P, SLOTS, D], BF16, name="tok%d" % t) for t in range(T)]
+        def load_k(t):
+            k_sb[t] = keep.tile([P, JB, D], BF16, tag="k_sb", name="k_sb")
+            nc.sync.dma_start(out=k_sb[t][:], in_=k_norm[t].rearrange("(jb p) c -> p jb c", p=P))
 
         def load_tok(t):
+            tok[t] = keep.tile([P, SLOTS, D], BF16, name="tok%d" % t)
             nc.sync.dma_start(
                 out=tok[t][:].rearrange("p (u e) c -> p u (e c)", u=2),
                 in_=updated_track_tokens[t].rearrange("(u p e) c -> p u (e c)", u=2, p=P),
             )
 
-        bias_t = [keep.tile([P, JB, HW], F32, name="bias_t%d" % t) for t in range(T)]
+        w_sb = keep.tile([P, D // P, D], BF16)
+        load_k(0)
+        load_q(0)
+        load_tok(0)
+        nc.sync.dma_start(out=w_sb[:], in_=W_out.rearrange("(ob p) c -> p ob c", p=P))
+        load_q(1)
+        load_tok(1)
+        load_q(2)
+
         k_t = [keep.tile([P, H, M], BF16, name="k_t%d" % t) for t in range(T)]
         v_codes = [keep.tile([P, D], U32, name="v_codes%d" % t, align_bytes=64) for t in range(T)]
         v_scales = [keep.tile([P, D], U8, name="v_scales%d" % t, align_bytes=64) for t in range(T)]
         w_codes = keep.tile([P, 2, D], U32, align_bytes=64)
         w_scales = keep.tile([P, 2, D], U8, align_bytes=64)
-        q_t = {}
-        v_grouped = {}
 
-        ident_bf = const.tile([P, P], BF16)
-        ident_f = const.tile([P, P], F32)
+        ident_bf = keep.tile([P, P], BF16)
+        ident_f = keep.tile([P, P], F32)
+        make_identity(nc, ident_bf[:])
+        make_identity(nc, ident_f[:])
+
+        quarter = keep.tile([P, 1], F32)
+        nc.vector.memset(quarter[:], 1.0)
+        nc.vector.tensor_scalar_mul(out=quarter[:], in0=quarter[:], scalar1=math.pi / 2.0)
+        first = keep.tile([P, 1], F32)
+        nc.scalar.activation(out=first[:], in_=quarter[:], func=ACT.Sin, scale=1.0)
+        theta = keep.tile([P, THETAS], F32)
+        nc.vector.memset(theta[:, 0:1], 1.0)
+        for doubling in range(8):
+            width = 2**doubling
+            nc.vector.tensor_scalar_mul(
+                out=theta[:, width : 2 * width], in0=theta[:, 0:width], scalar1=100.0 ** (-width / THETAS)
+            )
+        turns = keep.tile([P, T, 2, SLOTS], F32)
+        nc.vector.tensor_scalar_mul(
+            out=turns[:], in0=trk_v[:].rearrange("p t s c -> p t c s"), scalar1=1.0 / TURN
+        )
+
+        TERMS = 5
+        f_terms = keep.tile([P, IT, P], BF16)
+        t_terms = keep.tile([P, T * JB, P], BF16)
+        f_rows = keep.tile([P, IT, P], BF16)
+        t_rows = keep.tile([P, T * JB, P], BF16)
+
+        for terms in (f_terms, t_terms):
+            nc.gpsimd.memset(terms[:], 0.0)
+            nc.gpsimd.memset(terms[:, :, 0 : 2 * TERMS], 1.0)
+
+        def position_terms():
+            square = {}
+            for terms, position, square_at, linear_at, factor in (
+                (f_terms, fpos, 0, 2, -2.0),
+                (t_terms, trk_j, 3, 2, 1.0),
+            ):
+                at_term = terms[:, :, 0 : 2 * TERMS].rearrange("p n (c k) -> p n c k", c=2)
+                square[square_at] = (at_term, position, keep.tile(list(position.shape), F32, name="sq%d" % square_at))
+                nc.vector.tensor_tensor(out=square[square_at][2][:], in0=position[:], in1=position[:], op=ALU.mult)
+                nc.vector.tensor_scalar_mul(out=at_term[:, :, :, linear_at], in0=position[:], scalar1=factor)
+            for square_at, (at_term, position, sq) in square.items():
+                nc.vector.tensor_copy(out=at_term[:, :, :, square_at], in_=sq[:])
+            for square_at, (at_term, position, sq) in square.items():
+                nc.vector.tensor_tensor(
+                    out=at_term[:, :, :, square_at + 1], in0=sq[:], in1=at_term[:, :, :, square_at], op=ALU.subtract
+                )
+
+        def transpose_terms(terms, rows, count):
+            rows_ps = psum_t.tile([P, count, P], BF16, tag="tp", name="rows_ps")
+            for n in range(count):
+                nc.tensor.transpose(out=rows_ps[:, n, :], in_=terms[:, n, :], identity=ident_bf[:])
+            nc.scalar.copy(out=rows[:], in_=rows_ps[:])
+
+        d2_ps, bias = {}, {}
+
+        def square_distances(chunk, pair):
+            t, part = divmod(chunk * CHUNK // P, IT)
+            d2_ps[chunk, pair] = psum_t.tile([P, 2, CHUNK], F32, tag="tp", name="d2_ps")
+            for b in range(2):
+                nc.tensor.matmul(
+                    out=d2_ps[chunk, pair][:, b, :],
+                    lhsT=t_rows[:, t * JB + 2 * pair + b, :],
+                    rhs=f_rows[:, part : part + CHUNK // P, :].rearrange("p n i -> p (n i)"),
+                    start=True,
+                    stop=True,
+                )
+
+        def scale_bias(chunk, pair):
+            if pair == 0:
+                bias[chunk] = work.tile([P, JB, CHUNK], F32, tag="bias", name="bias", bufs=3)
+            target = bias[chunk][:, 2 * pair : 2 * pair + 2, :]
+            if pair == 0:
+                nc.scalar.activation(out=target, in_=d2_ps[chunk, pair][:], func=ACT.Copy, scale=-BIAS_GAIN)
+            else:
+                nc.vector.tensor_scalar_mul(out=target, in0=d2_ps[chunk, pair][:], scalar1=-BIAS_GAIN)
+
+        kt_ps = {}
+
+        def transpose_key(t, h):
+            kt_ps[t, h] = psum_t.tile([P, JB, P], BF16, tag="tp", name="kt_ps")
+            for jb in range(JB):
+                nc.tensor.transpose(
+                    out=kt_ps[t, h][:, jb, :], in_=k_sb[t][:, jb, cols(h, DH)], identity=ident_bf[:]
+                )
+
+        def copy_key(t, h):
+            target = k_t[t][:, h, :].rearrange("p (jb j) -> p jb j", jb=JB)
+            if t == 0:
+                nc.scalar.copy(out=target, in_=kt_ps[t, h][:])
+            else:
+                nc.vector.tensor_copy(out=target, in_=kt_ps[t, h][:])
+
+        qt_ps = {}
 
         def transpose_q(r):
-            qt_ps = psum_t.tile([P, H, P], BF16, tag="tp", name="qt_ps")
+            qt_ps[r] = psum_t.tile([P, H, P], BF16, tag="tp", name="qt_ps")
             for h in range(H):
-                nc.tensor.transpose(out=qt_ps[:, h, :], in_=q_tiles[r][:, cols(h, DH)], identity=ident_bf[:])
-            return qt_ps
+                nc.tensor.transpose(out=qt_ps[r][:, h, :], in_=q_sb[r][:, cols(h, DH)], identity=ident_bf[:])
 
-        with tc.tile_pool(name="prep", bufs=1) as prep:
-            k_sb = {}
-
-            def load_k(t):
-                k_sb[t] = prep.tile([P, JB, D], BF16, tag="k_sb", name="k_sb%d" % t)
-                nc.sync.dma_start(out=k_sb[t][:], in_=k_norm[t].rearrange("(jb p) c -> p jb c", p=P))
-
-            w_sb = prep.tile([P, D // P, D], BF16)
-            load_k(0)
-            load_q(0)
-            load_tok(0)
-            nc.sync.dma_start(out=w_sb[:], in_=W_out.rearrange("(ob p) c -> p ob c", p=P))
-            load_tok(1)
-            load_q(1)
-            load_q(2)
-
-            make_identity(nc, ident_bf[:])
-            make_identity(nc, ident_f[:])
-
-            theta = const.tile([P, PAIRS], F32)
-            nc.vector.memset(theta[:, 0:1], 1.0)
-            for doubling in range(8):
-                width = 2**doubling
-                nc.vector.tensor_scalar_mul(
-                    out=theta[:, width : 2 * width], in0=theta[:, 0:width], scalar1=100.0 ** (-width / PAIRS)
-                )
-            neg_trk = const.tile([P, T * JB, 2], F32)
-            nc.vector.tensor_scalar_mul(out=neg_trk[:], in0=trk_j[:], scalar1=-1.0)
-            turns = const.tile([P, T, 2, SLOTS], F32)
-            nc.vector.tensor_scalar_mul(
-                out=turns[:], in0=trk_v[:].rearrange("p t s c -> p t c s"), scalar1=1.0 / TURN
-            )
-            quarter = const.tile([P, 1], F32)
-            nc.vector.memset(quarter[:], 1.0)
-            nc.vector.tensor_scalar_mul(out=quarter[:], in0=quarter[:], scalar1=math.pi / 2.0)
-            fxy = fpos[:].rearrange("p (i c) -> p c i", c=2)
-            squares = {}
-
-            def square_distances(t, jb):
-                for c in range(2):
-                    squares[t, jb, c] = prep.tile([P, HW], F32, tag="square%d" % c, name="square%d" % c, bufs=2)
-                    nc.scalar.activation(
-                        out=squares[t, jb, c][:],
-                        in_=fxy[:, c, :],
-                        func=ACT.Square,
-                        bias=neg_trk[:, t * JB + jb, c : c + 1],
-                        scale=1.0,
-                    )
-
-            def finish_bias(t, jb):
-                dx2, dy2 = squares[t, jb, 0], squares[t, jb, 1]
-                nc.vector.tensor_tensor(out=dx2[:], in0=dx2[:], in1=dy2[:], op=ALU.add)
-                nc.vector.tensor_scalar_mul(out=bias_t[t][:, jb, :], in0=dx2[:], scalar1=-BIAS_GAIN)
-
-            def bias_on_gpsimd(t, jb):
-                apart = [values.tile([P, HW], F32, tag="apart%d" % c, name="apart%d" % c) for c in range(2)]
-                for c in range(2):
-                    nc.gpsimd.tensor_scalar(
-                        out=apart[c][:],
-                        in0=fxy[:, c, :],
-                        scalar1=1.0,
-                        scalar2=neg_trk[:, t * JB + jb, c : c + 1],
-                        op0=ALU.mult,
-                        op1=ALU.add,
-                    )
-                    nc.gpsimd.tensor_tensor(out=apart[c][:], in0=apart[c][:], in1=apart[c][:], op=ALU.mult)
-                nc.gpsimd.tensor_tensor(out=apart[0][:], in0=apart[0][:], in1=apart[1][:], op=ALU.add)
-                nc.gpsimd.tensor_scalar(
-                    out=bias_t[t][:, jb, :], in0=apart[0][:], scalar1=-BIAS_GAIN, scalar2=0.0, op0=ALU.mult, op1=ALU.add
-                )
-
-            def transpose_keys(t, hp):
-                kt_ps = psum_t.tile([P, 2, JB, P], BF16, tag="tp", name="kt_ps")
-                for hh in range(2):
-                    for jb in range(JB):
-                        nc.tensor.transpose(
-                            out=kt_ps[:, hh, jb, :], in_=k_sb[t][:, jb, cols(2 * hp + hh, DH)], identity=ident_bf[:]
-                        )
-                nc.vector.tensor_copy(
-                    out=k_t[t][:, 2 * hp : 2 * hp + 2, :].rearrange("p h (jb j) -> p h jb j", jb=JB), in_=kt_ps[:]
-                )
-
-            table = {}
-
-            def angle_tables(t, half):
-                shape = [P, PAIRS, SLOTS]
-                u = prep.tile(shape, F32, tag="u")
-                nc.vector.tensor_tensor(
-                    out=u[:],
-                    in0=theta[:].unsqueeze(2).to_broadcast(shape),
-                    in1=turns[:, t, half, :].unsqueeze(1).to_broadcast(shape),
-                    op=ALU.mult,
-                )
-                back = prep.tile(shape, F32, tag="back")
-                nc.vector.tensor_scalar_add(out=back[:], in0=u[:], scalar1=ROUND_MAGIC)
-                nc.vector.scalar_tensor_tensor(
-                    out=back[:], in0=back[:], scalar=ROUND_MAGIC, in1=u[:], op0=ALU.subtract, op1=ALU.subtract
-                )
-                fold = prep.tile(shape, F32, tag="fold")
-                nc.vector.scalar_tensor_tensor(
-                    out=fold[:], in0=back[:], scalar=-1.0, in1=back[:], op0=ALU.mult, op1=ALU.min
-                )
-                table[t, half] = values.tile([P, 3, PAIRS, SLOTS], F32, name="table%d%d" % (t, half))
-                nc.scalar.activation(
-                    out=table[t, half][:, 1, :, :], in_=fold[:], func=ACT.Sin, bias=quarter[:, 0:1], scale=TURN
-                )
-                nc.scalar.activation(out=table[t, half][:, 2, :, :], in_=back[:], func=ACT.Sin, scale=-TURN)
-
-            def rotate_values(t, half):
-                tab = table[t, half]
-                nc.gpsimd.tensor_scalar(
-                    out=tab[:, 0, :, :], in0=tab[:, 2, :, :], scalar1=-1.0, scalar2=0.0, op0=ALU.mult, op1=ALU.add
-                )
-                ab = tok[t][:, :, cols(half, 2 * PAIRS)].rearrange("p s (i w) -> p w i s", w=2)
-                full = [P, PAIRS, 2, SLOTS]
-                part_a = values.tile(full, F32, tag="part_a")
-                part_b = values.tile(full, F32, tag="part_b")
-                nc.gpsimd.tensor_tensor(
-                    out=part_a[:],
-                    in0=ab[:, 0, :, :].unsqueeze(2).to_broadcast(full),
-                    in1=tab[:, 1:3, :, :].rearrange("p w i s -> p i w s"),
-                    op=ALU.mult,
-                )
-                nc.gpsimd.tensor_tensor(
-                    out=part_b[:],
-                    in0=ab[:, 1, :, :].unsqueeze(2).to_broadcast(full),
-                    in1=tab[:, 0:2, :, :].rearrange("p w i s -> p i w s"),
-                    op=ALU.mult,
-                )
-                v_grouped[t, half] = values.tile(full, BF16, name="v_grouped%d%d" % (t, half), align_bytes=64)
-                nc.gpsimd.tensor_tensor(out=v_grouped[t, half][:], in0=part_a[:], in1=part_b[:], op=ALU.add)
-
-            def quantise_weights(g):
-                w_grouped = prep.tile([P, D, 2], F32, tag="w_grouped", align_bytes=64)
-                for op in range(4):
-                    wt_ps = psum_t.tile([P, 2, 2, P], F32, tag="tp", name="wt_ps")
-                    for u in range(2):
-                        for ob in range(2):
-                            nc.tensor.transpose(
-                                out=wt_ps[:, u, ob, :],
-                                in_=w_sb[:, 2 * op + ob, :].bitcast(F32)[:, cols(2 * g + u, P)],
-                                identity=ident_f[:],
-                            )
-                    nc.scalar.copy(
-                        out=w_grouped[:, cols(op, 2 * P), :], in_=wt_ps[:].rearrange("p u ob o -> p (ob o) u")
-                    )
-                nc.vector.quantize_mx(
-                    out=w_codes[:, g, :].bitcast(FP8X4),
-                    scales=w_scales[:, g, :],
-                    in_=w_grouped[:].rearrange("p o u -> p (o u)").bitcast(BF16),
-                )
-
-            square_distances(0, 0)
-            square_distances(0, 1)
-            angle_tables(0, 0)
-            rotate_values(0, 0)
-            finish_bias(0, 0)
-            finish_bias(0, 1)
-            square_distances(0, 2)
-            square_distances(0, 3)
-            angle_tables(0, 1)
-            rotate_values(0, 1)
-            finish_bias(0, 2)
-            finish_bias(0, 3)
-            for hp in range(H // 2):
-                transpose_keys(0, hp)
-            load_k(1)
-            for jb in range(JB):
-                bias_on_gpsimd(1, jb)
-            for half in range(2):
-                angle_tables(1, half)
-                rotate_values(1, half)
-            for hp in range(H // 2):
-                transpose_keys(1, hp)
-            for g in range(2):
-                quantise_weights(g)
-
-        work = stack.enter_context(tc.tile_pool(name="work", bufs=2))
-        sc_of, shift_of, e_of, et_of, eg_of = {}, {}, {}, {}, {}
-        rowsum_of, codes_of, scales_of, pv_of, sampled_of, st_of, sg_of, po_of = {}, {}, {}, {}, {}, {}, {}, {}
-
-        def copy_q(r, qt_ps):
+        def copy_q(r):
             q_t[r] = work.tile([P, H, P], BF16, tag="q_t", name="q_t")
-            nc.scalar.copy(out=q_t[r][:], in_=qt_ps[:])
+            nc.scalar.copy(out=q_t[r][:], in_=qt_ps[r][:])
 
-        def scores(n):
-            r, h = divmod(n, H)
-            t, it = divmod(r, IT)
-            sc_of[n] = psum_s.tile([P, M], F32, tag="sc", name="sc")
-            for jb in range(JB):
-                nc.tensor.matmul(
-                    out=sc_of[n][:, cols(jb, P)],
-                    lhsT=bias_t[t][:, jb, cols(it, P)],
-                    rhs=ident_f[:],
-                    is_transpose=True,
-                    start=(jb == 0),
-                    stop=False,
+        back, fold, table, v_grouped = {}, {}, {}, {}
+        grid = [P, SLOTS, THETAS]
+
+        def angles(t, half):
+            whole = work.tile(grid, I32, tag="whole", bufs=1)
+            for s in range(SLOTS):
+                nc.vector.tensor_scalar(
+                    out=whole[:, s, :], in0=theta[:], scalar1=turns[:, t, half, s : s + 1], scalar2=None, op0=ALU.mult
                 )
-            nc.tensor.matmul(out=sc_of[n][:], lhsT=q_t[r][:, h, :], rhs=k_t[t][:, h, :], start=False, stop=True)
+            back[t, half] = work.tile(grid, F32, tag="back", name="back")
+            for s in range(SLOTS):
+                nc.vector.scalar_tensor_tensor(
+                    out=back[t, half][:, s, :],
+                    in0=theta[:],
+                    scalar=turns[:, t, half, s : s + 1],
+                    in1=whole[:, s, :],
+                    op0=ALU.mult,
+                    op1=ALU.subtract,
+                )
+            fold[t, half] = work.tile(grid, F32, tag="fold", name="fold")
+            nc.vector.scalar_tensor_tensor(
+                out=fold[t, half][:], in0=back[t, half][:], scalar=-1.0, in1=back[t, half][:], op0=ALU.mult, op1=ALU.min
+            )
 
-        def row_shift(n):
-            shift_of[n] = stats.tile([P, 1], F32, tag="shift", name="shift")
+        def sines(t, half):
+            table[t, half] = keep.tile([P, 2, SLOTS, THETAS], F32, name="table%d%d" % (t, half))
+            nc.scalar.activation(
+                out=table[t, half][:, 0, :, :], in_=fold[t, half][:], func=ACT.Sin, bias=quarter[:, 0:1], scale=TURN
+            )
+            nc.scalar.activation(out=table[t, half][:, 1, :, :], in_=back[t, half][:], func=ACT.Sin, scale=TURN)
+
+        def rotate_values(t, half):
+            pair = tok[t][:, :, cols(half, 2 * THETAS)].rearrange("p s (i w) -> p w s i", w=2)
+            v_grouped[t, half] = work.tile(
+                [P, THETAS, 2, SLOTS], BF16, tag="v_grouped", name="v_grouped", align_bytes=64
+            )
+            for piece in range(THETAS // PIECE):
+                part = cols(piece, PIECE)
+                product = {}
+                for w in range(2):
+                    for which in range(2):
+                        product[w, which] = work.tile(
+                            [P, SLOTS, PIECE], F32, tag="product%d%d" % (w, which), name="product"
+                        )
+                        nc.gpsimd.tensor_tensor(
+                            out=product[w, which][:],
+                            in0=pair[:, w, :, part],
+                            in1=table[t, half][:, which, :, part],
+                            op=ALU.mult,
+                        )
+                for w, op in ((0, ALU.subtract), (1, ALU.add)):
+                    nc.gpsimd.tensor_tensor(
+                        out=v_grouped[t, half][:, part, w, :],
+                        in0=product[0, w][:].rearrange("p s i -> p i s"),
+                        in1=product[1, 1 - w][:].rearrange("p s i -> p i s"),
+                        op=op,
+                    )
+
+        def quantise_values(t, half):
+            nc.vector.quantize_mx(
+                out=v_codes[t][:, cols(half, 2 * THETAS)].bitcast(FP8X4),
+                scales=v_scales[t][:, cols(half, 2 * THETAS)],
+                in_=v_grouped[t, half][:].rearrange("p i w s -> p (i w s)"),
+            )
+
+        w_grouped, wt_ps = {}, {}
+
+        def transpose_weights(g, op):
+            wt_ps[g, op] = psum_t.tile([P, 2, 2, P], F32, tag="tp", name="wt_ps")
+            for u in range(2):
+                for ob in range(2):
+                    nc.tensor.transpose(
+                        out=wt_ps[g, op][:, u, ob, :],
+                        in_=w_sb[:, 2 * op + ob, :].bitcast(F32)[:, cols(2 * g + u, P)],
+                        identity=ident_f[:],
+                    )
+
+        def regroup_weights(g, op):
+            if op == 0:
+                w_grouped[g] = work.tile([P, D, 2], F32, tag="w_grouped", name="w_grouped", align_bytes=64, bufs=1)
+            nc.scalar.copy(
+                out=w_grouped[g][:, cols(op, 2 * P), :], in_=wt_ps[g, op][:].rearrange("p u ob o -> p (ob o) u")
+            )
+
+        def quantise_weights(g):
+            nc.vector.quantize_mx(
+                out=w_codes[:, g, :].bitcast(FP8X4),
+                scales=w_scales[:, g, :],
+                in_=w_grouped[g][:].rearrange("p o u -> p (o u)").bitcast(BF16),
+            )
+
+        score, shift, e_of, et_of, eg_of = {}, {}, {}, {}, {}
+        rowsum, codes, scales, pv, sampled, st_of, sg_of, sq_of, po, o_sb = {}, {}, {}, {}, {}, {}, {}, {}, {}, {}
+
+        def begin_scores(m):
+            r = m // DUOS
+            chunk, part = divmod(r * P, CHUNK)
+            for hh in range(2):
+                score[m, hh] = psum_s.tile([P, M], F32, tag="sc", name="sc")
+                for jb in range(JB):
+                    nc.tensor.matmul(
+                        out=score[m, hh][:, cols(jb, P)],
+                        lhsT=bias[chunk][:, jb, part : part + P],
+                        rhs=ident_f[:],
+                        is_transpose=True,
+                        start=(jb == 0),
+                        stop=False,
+                    )
+
+        def finish_scores(m):
+            r, hp = divmod(m, DUOS)
+            for hh in range(2):
+                h = 2 * hp + hh
+                nc.tensor.matmul(
+                    out=score[m, hh][:], lhsT=q_t[r][:, h, :], rhs=k_t[r // IT][:, h, :], start=False, stop=True
+                )
+
+        def row_shift(m, hh):
+            shift[m, hh] = work.tile([P, 1], F32, tag="shift", name="shift", bufs=6)
             unread = work.tile([P, M], BF16, tag="unread")
             nc.vector.tensor_scalar(
                 out=unread[:],
-                in0=sc_of[n][:],
+                in0=score[m, hh][:],
                 scalar1=-SCALE,
                 scalar2=None,
                 op0=ALU.mult,
                 op1=ALU.min,
-                accum_out=shift_of[n][:],
+                accum_out=shift[m, hh][:],
             )
 
-        def exponent(n):
-            r, h = divmod(n, H)
-            if h == 0:
-                rowsum_of[r] = stats.tile([P, H], F32, tag="rowsum", name="rowsum")
-            if n % 2 == 0:
-                e_of[n // 2] = work.tile([P, 2, M], BF16, tag="e_sb", name="e_sb", bufs=4)
+        def exponent(m, hh):
+            r, hp = divmod(m, DUOS)
+            if hp == 0 and hh == 0:
+                rowsum[r] = work.tile([P, H], F32, tag="rowsum", name="rowsum", bufs=6)
+            if hh == 0:
+                e_of[m] = work.tile([P, 2, M], BF16, tag="e_sb", name="e_sb", bufs=4)
             nc.scalar.activation(
-                out=e_of[n // 2][:, n % 2, :],
-                in_=sc_of[n][:],
+                out=e_of[m][:, hh, :],
+                in_=score[m, hh][:],
                 func=ACT.Exp,
-                bias=shift_of[n][:],
+                bias=shift[m, hh][:],
                 scale=SCALE,
-                accum_out=rowsum_of[r][:, h : h + 1],
+                accum_out=rowsum[r][:, 2 * hp + hh : 2 * hp + hh + 1],
             )
 
         def transpose_e(m):
@@ -342,55 +364,48 @@ def tile_attentionalsplatting_pb_kernel(
             nc.scalar.copy(out=eg_of[m][:], in_=et_of[m][:].rearrange("p h u i -> p h i u"))
 
         def quantise_e(m):
-            r, hp = divmod(m, H // 2)
+            r, hp = divmod(m, DUOS)
             if hp == 0:
-                codes_of[r] = work.tile([P, H * P], U32, tag="e_codes", name="e_codes", align_bytes=64)
-                scales_of[r] = work.tile([P, H * P], U8, tag="e_scales", name="e_scales", align_bytes=64)
+                codes[r] = work.tile([P, H * P], U32, tag="e_codes", name="e_codes", align_bytes=64, bufs=3)
+                scales[r] = work.tile([P, H * P], U8, tag="e_scales", name="e_scales", align_bytes=64, bufs=3)
             nc.vector.quantize_mx(
-                out=codes_of[r][:, cols(hp, 2 * P)].bitcast(FP8X4),
-                scales=scales_of[r][:, cols(hp, 2 * P)],
+                out=codes[r][:, cols(hp, 2 * P)].bitcast(FP8X4),
+                scales=scales[r][:, cols(hp, 2 * P)],
                 in_=eg_of[m][:].rearrange("p h i u -> p (h i u)").bitcast(BF16),
             )
 
-        def quantise_values(t):
-            for half in range(2):
-                nc.vector.quantize_mx(
-                    out=v_codes[t][:, cols(half, 2 * PAIRS)].bitcast(FP8X4),
-                    scales=v_scales[t][:, cols(half, 2 * PAIRS)],
-                    in_=v_grouped[t, half][:].rearrange("p i w s -> p (i w s)"),
-                )
-
-        def multiply_values(r):
+        def multiply_values(r, half):
             t = r // IT
-            for half in range(2):
-                pv_of[r, half] = psum_m.tile([P, 4, DH], F32, tag="mm", name="pv")
-                for hq in range(4):
-                    h = 4 * half + hq
-                    nc.tensor.matmul_mx(
-                        out=pv_of[r, half][:, hq, :],
-                        lhsT=codes_of[r][:, cols(h, P)].bitcast(FP8X4),
-                        lhsT_scale=scales_of[r][:, cols(h, P)],
-                        rhs=v_codes[t][:, cols(h, DH)].bitcast(FP8X4),
-                        rhs_scale=v_scales[t][:, cols(h, DH)],
-                        start=True,
-                        stop=True,
-                    )
-
-        def normalise(r):
-            inv_sum = stats.tile([P, H], F32, tag="inv_sum")
-            nc.vector.reciprocal(out=inv_sum[:], in_=rowsum_of[r][:])
-            sampled_of[r] = work.tile([P, 2, 4, DH], BF16, tag="sampled", name="sampled")
-            for half in range(2):
-                nc.vector.tensor_tensor(
-                    out=sampled_of[r][:, half, :, :],
-                    in0=pv_of[r, half][:],
-                    in1=inv_sum[:, cols(half, 4)].unsqueeze(2).to_broadcast([P, 4, DH]),
-                    op=ALU.mult,
+            pv[r, half] = psum_m.tile([P, 4, DH], F32, tag="mm", name="pv")
+            for hq in range(4):
+                h = 4 * half + hq
+                nc.tensor.matmul_mx(
+                    out=pv[r, half][:, hq, :],
+                    lhsT=codes[r][:, cols(h, P)].bitcast(FP8X4),
+                    lhsT_scale=scales[r][:, cols(h, P)],
+                    rhs=v_codes[t][:, cols(h, DH)].bitcast(FP8X4),
+                    rhs_scale=v_scales[t][:, cols(h, DH)],
+                    start=True,
+                    stop=True,
                 )
+
+        inv_sum = {}
+
+        def normalise(r, half):
+            if half == 0:
+                inv_sum[r] = work.tile([P, H], F32, tag="inv_sum", name="inv_sum")
+                nc.vector.reciprocal(out=inv_sum[r][:], in_=rowsum[r][:])
+                sampled[r] = work.tile([P, 2, 4, DH], BF16, tag="sampled", name="sampled")
+            nc.vector.tensor_tensor(
+                out=sampled[r][:, half, :, :],
+                in0=pv[r, half][:],
+                in1=inv_sum[r][:, cols(half, 4)].unsqueeze(2).to_broadcast([P, 4, DH]),
+                op=ALU.mult,
+            )
 
         def transpose_sampled(r):
             st_of[r] = psum_t.tile([P, 2, 2, P], F32, tag="tp", name="st_ps")
-            words = sampled_of[r][:].rearrange("p a b c -> p (a b c)").bitcast(F32)
+            words = sampled[r][:].rearrange("p a b c -> p (a b c)").bitcast(F32)
             for g in range(2):
                 for u in range(2):
                     nc.tensor.transpose(out=st_of[r][:, g, u, :], in_=words[:, cols(2 * g + u, P)], identity=ident_f[:])
@@ -400,73 +415,130 @@ def tile_attentionalsplatting_pb_kernel(
             nc.scalar.copy(out=sg_of[r][:], in_=st_of[r][:].rearrange("p g u i -> p g i u"))
 
         def quantise_sampled(r):
-            s_codes = work.tile([P, 2 * P], U32, tag="s_codes", align_bytes=64)
-            s_scales = work.tile([P, 2 * P], U8, tag="s_scales", align_bytes=64)
+            s_codes = work.tile([P, 2 * P], U32, tag="s_codes", align_bytes=64, bufs=3)
+            s_scales = work.tile([P, 2 * P], U8, tag="s_scales", align_bytes=64, bufs=3)
             nc.vector.quantize_mx(
                 out=s_codes[:].bitcast(FP8X4),
                 scales=s_scales[:],
                 in_=sg_of[r][:].rearrange("p g i u -> p (g i u)").bitcast(BF16),
             )
-            sg_of[r] = (s_codes, s_scales)
+            sq_of[r] = (s_codes, s_scales)
 
-        def project(r):
-            s_codes, s_scales = sg_of[r]
-            for nh in range(2):
-                po_of[r, nh] = psum_m.tile([P, 512], F32, tag="mm", name="po")
-                for g in range(2):
-                    nc.tensor.matmul_mx(
-                        out=po_of[r, nh][:],
-                        lhsT=s_codes[:, cols(g, P)].bitcast(FP8X4),
-                        lhsT_scale=s_scales[:, cols(g, P)],
-                        rhs=w_codes[:, g, cols(nh, 512)].bitcast(FP8X4),
-                        rhs_scale=w_scales[:, g, cols(nh, 512)],
-                        start=(g == 0),
-                        stop=(g == 1),
-                    )
+        def project(r, nh):
+            s_codes, s_scales = sq_of[r]
+            po[r, nh] = psum_m.tile([P, 512], F32, tag="mm", name="po")
+            for g in range(2):
+                nc.tensor.matmul_mx(
+                    out=po[r, nh][:],
+                    lhsT=s_codes[:, cols(g, P)].bitcast(FP8X4),
+                    lhsT_scale=s_scales[:, cols(g, P)],
+                    rhs=w_codes[:, g, cols(nh, 512)].bitcast(FP8X4),
+                    rhs_scale=w_scales[:, g, cols(nh, 512)],
+                    start=(g == 0),
+                    stop=(g == 1),
+                )
 
-        def store(r):
+        def store(r, nh):
             t, it = divmod(r, IT)
-            o_sb = work.tile([P, D], F32, tag="o_sb")
-            for nh in range(2):
-                nc.scalar.copy(out=o_sb[:, cols(nh, 512)], in_=po_of[r, nh][:])
-            nc.sync.dma_start(out=out[t, cols(it, P), :], in_=o_sb[:])
+            o_sb = work.tile([P, 512], F32, tag="o_sb", bufs=3)
+            if nh == 0:
+                nc.scalar.copy(out=o_sb[:], in_=po[r, nh][:])
+            else:
+                nc.vector.tensor_copy(out=o_sb[:], in_=po[r, nh][:])
+            nc.sync.dma_start(out=out[t, cols(it, P), cols(nh, 512)], in_=o_sb[:])
 
-        heads = ROUNDS * H
-        copy_q(0, transpose_q(0))
+        for h in range(H // 2):
+            transpose_key(0, h)
+            copy_key(0, h)
+        position_terms()
+        transpose_terms(f_terms, f_rows, IT)
+        transpose_terms(t_terms, t_rows, T * JB)
+        angles(0, 0)
+        angles(0, 1)
+        transpose_q(0)
+        copy_q(0)
+        square_distances(0, 0)
+        scale_bias(0, 0)
+        sines(0, 0)
+        square_distances(0, 1)
+        scale_bias(0, 1)
+        for h in range(H // 2, H):
+            transpose_key(0, h)
+            copy_key(0, h)
+        load_k(1)
         load_q(3)
-        next_q = {}
-        for n in range(heads + 24):
-            r, step = divmod(n, H)
-            if step == 2 and 0 <= r - 2 < ROUNDS:
-                transpose_sampled(r - 2)
-            if n % 2 == 0 and 0 <= (n - 6) // 2 < heads // 2:
-                transpose_e((n - 6) // 2)
-            if step == 5 and r + 1 < ROUNDS:
-                next_q[r + 1] = transpose_q(r + 1)
-                load_q(r + 4)
-            if n < heads:
-                scores(n)
-            if step == 7 and 0 <= r - 1 < ROUNDS:
-                multiply_values(r - 1)
-            if step == 5 and 0 <= r - 2 < ROUNDS:
-                project(r - 2)
-            if 0 <= n - 1 < heads:
-                row_shift(n - 1)
-            if 0 <= n - 2 < heads:
-                exponent(n - 2)
-            if n % 2 == 1 and 0 <= (n - 7) // 2 < heads // 2:
-                regroup_e((n - 7) // 2)
-            if n % 2 == 0 and 0 <= (n - 8) // 2 < heads // 2:
-                quantise_e((n - 8) // 2)
-            if step == 6 and r + 1 < ROUNDS:
-                copy_q(r + 1, next_q[r + 1])
-            if step == 5 and 0 <= r - 1 < ROUNDS and (r - 1) % IT == 0:
-                quantise_values((r - 1) // IT)
-            if step == 0 and 0 <= r - 2 < ROUNDS:
-                normalise(r - 2)
-            if step == 3 and 0 <= r - 2 < ROUNDS:
-                regroup_sampled(r - 2)
-            if step == 4 and 0 <= r - 2 < ROUNDS:
-                quantise_sampled(r - 2)
-            if step == 6 and 0 <= r - 2 < ROUNDS:
-                store(r - 2)
+        sines(0, 1)
+        rotate_values(0, 0)
+        rotate_values(0, 1)
+        for half in range(2):
+            angles(1, half)
+            sines(1, half)
+            rotate_values(1, half)
+        nc.scalar.activation(out=first[:], in_=quarter[:], func=ACT.Exp, scale=1.0)
+
+        due = {}
+
+        def at(step, work_on, *which):
+            due.setdefault(step, []).append((work_on, which))
+
+        for r in range(ROUNDS):
+            start = max(DUOS * r + 6, VALUES_STEP + 2 * r)
+            second = start + (2 if start == DUOS * r + 6 else 1)
+            for half, step in ((0, start), (1, second)):
+                at(step, multiply_values, r, half)
+                at(step + 1, normalise, r, half)
+            at(second + 2, transpose_sampled, r)
+            at(second + 2, regroup_sampled, r)
+            at(second + 3, quantise_sampled, r)
+            last = r == ROUNDS - 1
+            steady = second == start + 2
+            for nh, step in ((0, second + (4 if last else 5)), (1, second + (4 if last else 7 if steady else 6))):
+                at(step, project, r, nh)
+                at(step + 1, store, r, nh)
+            if r + 1 < ROUNDS:
+                at(DUOS * r + 1, transpose_q, r + 1)
+                at(DUOS * r + 1, copy_q, r + 1)
+                at(DUOS * r + 1, load_q, r + 4)
+        for chunk in range(1, CHUNKS):
+            for pair in range(2):
+                at(8 * chunk - 5 + 2 * pair, square_distances, chunk, pair)
+                at(8 * chunk - 5 + 2 * pair, scale_bias, chunk, pair)
+        for g in range(2):
+            for op in range(4):
+                at(4 + 4 * g + op, transpose_weights, g, op)
+                at(4 + 4 * g + op, regroup_weights, g, op)
+            at(8 + 4 * g, quantise_weights, g)
+        for h in range(H):
+            at(12 + h, transpose_key, 1, h)
+            at(12 + h, copy_key, 1, h)
+        for half in range(2):
+            at(VALUES_STEP - 2 + half, quantise_values, 0, half)
+            at(DUOS * IT + 4 + half, quantise_values, 1, half)
+
+        def run(step, *kinds):
+            for kind in kinds:
+                for work_on, which in due.get(step, []):
+                    if work_on == kind:
+                        work_on(*which)
+
+        for n in range(max(due) + 1):
+            if 0 <= n - 3 < STEPS:
+                transpose_e(n - 3)
+            if 0 <= n - 1 < STEPS:
+                row_shift(n - 1, 0)
+                exponent(n - 1, 0)
+                row_shift(n - 1, 1)
+            if 0 <= n - 3 < STEPS:
+                regroup_e(n - 3)
+            if 0 <= n - 1 < STEPS:
+                exponent(n - 1, 1)
+            run(n, transpose_q, copy_q, load_q, transpose_sampled, regroup_sampled)
+            run(n, transpose_key, copy_key, transpose_weights, regroup_weights)
+            if n < STEPS:
+                begin_scores(n)
+                finish_scores(n)
+            run(n, square_distances, scale_bias, quantise_values)
+            if 0 <= n - 4 < STEPS:
+                quantise_e(n - 4)
+            run(n, normalise, quantise_sampled, quantise_weights, store)
+            run(n, multiply_values, project)

@@ -29,12 +29,12 @@ THETAS = 256
 SLOTS = 4
 CHUNK = 256
 CHUNKS = T * HW // CHUNK
-PIECE = 64
+PIECE = 128
 
 SCALE = 1.0 / math.sqrt(DH)
 BIAS_GAIN = 2.0 / SCALE
 TURN = 2.0 * math.pi
-VALUES_STEP = 12
+VALUES_STEP = 16
 
 FLOPS = 2 * (2 * T * H * HW * M * DH) + 2 * T * HW * D * D
 
@@ -52,10 +52,9 @@ def tile_attentionalsplatting_pb_kernel(
         keep = stack.enter_context(tc.tile_pool(name="keep", bufs=1))
         work = stack.enter_context(tc.tile_pool(name="work", bufs=2))
         psum_s = stack.enter_context(tc.psum_pool(name="psum_s", bufs=4))
-        psum_t = stack.enter_context(tc.psum_pool(name="psum_t", bufs=2))
-        psum_m = stack.enter_context(tc.psum_pool(name="psum_m", bufs=2))
+        psum_t = stack.enter_context(tc.psum_pool(name="psum_t", bufs=4))
 
-        trk_j = keep.tile([P, T * JB, 2], BF16)
+        trk_p = keep.tile([P, T, JB, 2], BF16)
         trk_v = keep.tile([P, T, SLOTS, 2], BF16)
         fpos = keep.tile([P, IT, 2], BF16)
         with nc.allow_non_contiguous_dma(reason="a few KiB of positions"):
@@ -63,8 +62,8 @@ def tile_attentionalsplatting_pb_kernel(
                 out=trk_v[:].rearrange("p t (u e) c -> p (t u) (e c)", u=2),
                 in_=tracks.rearrange("t (u p e) c -> p (t u) (e c)", u=2, p=P),
             )
-            nc.scalar.dma_start(out=trk_j[:], in_=tracks.rearrange("t (jb p) c -> p (t jb) c", p=P))
-            nc.scalar.dma_start(out=fpos[:], in_=feature_positions.rearrange("(it p) c -> p it c", p=P))
+            nc.sync.dma_start(out=fpos[:], in_=feature_positions.rearrange("(p n) c -> p n c", p=P))
+            nc.sync.dma_start(out=trk_p[:], in_=tracks.rearrange("t (p n) c -> p t n c", p=P))
 
         q_sb, k_sb, tok, q_t = {}, {}, {}, {}
 
@@ -124,8 +123,8 @@ def tile_attentionalsplatting_pb_kernel(
         TERMS = 5
         f_terms = keep.tile([P, IT, P], BF16)
         t_terms = keep.tile([P, T * JB, P], BF16)
-        f_rows = keep.tile([P, IT, P], BF16)
-        t_rows = keep.tile([P, T * JB, P], BF16)
+        f_rows = keep.tile([P, HW], BF16)
+        t_rows = keep.tile([P, T, M], BF16)
 
         for terms in (f_terms, t_terms):
             nc.gpsimd.memset(terms[:], 0.0)
@@ -134,13 +133,13 @@ def tile_attentionalsplatting_pb_kernel(
         def position_terms():
             square = {}
             for terms, position, square_at, linear_at, factor in (
-                (f_terms, fpos, 0, 2, -2.0),
-                (t_terms, trk_j, 3, 2, 1.0),
+                (f_terms, fpos[:], 0, 2, -2.0),
+                (t_terms, trk_p[:].rearrange("p t n c -> p (t n) c"), 3, 2, 1.0),
             ):
                 at_term = terms[:, :, 0 : 2 * TERMS].rearrange("p n (c k) -> p n c k", c=2)
                 square[square_at] = (at_term, position, keep.tile(list(position.shape), F32, name="sq%d" % square_at))
-                nc.vector.tensor_tensor(out=square[square_at][2][:], in0=position[:], in1=position[:], op=ALU.mult)
-                nc.vector.tensor_scalar_mul(out=at_term[:, :, :, linear_at], in0=position[:], scalar1=factor)
+                nc.vector.tensor_tensor(out=square[square_at][2][:], in0=position, in1=position, op=ALU.mult)
+                nc.vector.tensor_scalar_mul(out=at_term[:, :, :, linear_at], in0=position, scalar1=factor)
             for square_at, (at_term, position, sq) in square.items():
                 nc.vector.tensor_copy(out=at_term[:, :, :, square_at], in_=sq[:])
             for square_at, (at_term, position, sq) in square.items():
@@ -148,22 +147,25 @@ def tile_attentionalsplatting_pb_kernel(
                     out=at_term[:, :, :, square_at + 1], in0=sq[:], in1=at_term[:, :, :, square_at], op=ALU.subtract
                 )
 
-        def transpose_terms(terms, rows, count):
-            rows_ps = psum_t.tile([P, count, P], BF16, tag="tp", name="rows_ps")
-            for n in range(count):
+        def transpose_terms(terms, rows, frames, count):
+            rows_ps = psum_t.tile([P, frames * count, P], BF16, tag="tp", name="rows_ps")
+            for n in range(frames * count):
                 nc.tensor.transpose(out=rows_ps[:, n, :], in_=terms[:, n, :], identity=ident_bf[:])
-            nc.scalar.copy(out=rows[:], in_=rows_ps[:])
+            nc.scalar.copy(
+                out=rows.rearrange("k (t p n) -> k t p n", t=frames, n=count),
+                in_=rows_ps[:].rearrange("k (t n) p -> k t p n", t=frames),
+            )
 
         d2_ps, bias = {}, {}
 
         def square_distances(chunk, pair):
-            t, part = divmod(chunk * CHUNK // P, IT)
+            t, part = divmod(chunk * CHUNK, HW)
             d2_ps[chunk, pair] = psum_t.tile([P, 2, CHUNK], F32, tag="tp", name="d2_ps")
             for b in range(2):
                 nc.tensor.matmul(
                     out=d2_ps[chunk, pair][:, b, :],
-                    lhsT=t_rows[:, t * JB + 2 * pair + b, :],
-                    rhs=f_rows[:, part : part + CHUNK // P, :].rearrange("p n i -> p (n i)"),
+                    lhsT=t_rows[:, t, cols(2 * pair + b, P)],
+                    rhs=f_rows[:, part : part + CHUNK],
                     start=True,
                     stop=True,
                 )
@@ -204,36 +206,36 @@ def tile_attentionalsplatting_pb_kernel(
             q_t[r] = work.tile([P, H, P], BF16, tag="q_t", name="q_t")
             nc.scalar.copy(out=q_t[r][:], in_=qt_ps[r][:])
 
-        back, fold, table, v_grouped = {}, {}, {}, {}
+        angle, table, v_grouped = {}, {}, {}
         grid = [P, SLOTS, THETAS]
 
         def angles(t, half):
-            whole = work.tile(grid, I32, tag="whole", bufs=1)
+            whole = work.tile(grid, I32, tag="bias", bufs=3)
             for s in range(SLOTS):
                 nc.vector.tensor_scalar(
                     out=whole[:, s, :], in0=theta[:], scalar1=turns[:, t, half, s : s + 1], scalar2=None, op0=ALU.mult
                 )
-            back[t, half] = work.tile(grid, F32, tag="back", name="back")
+            angle[t, half] = work.tile([P, 2, SLOTS, THETAS], F32, tag="angle", name="angle", align_bytes=64)
             for s in range(SLOTS):
                 nc.vector.scalar_tensor_tensor(
-                    out=back[t, half][:, s, :],
+                    out=angle[t, half][:, 0, s, :],
                     in0=theta[:],
                     scalar=turns[:, t, half, s : s + 1],
                     in1=whole[:, s, :],
                     op0=ALU.mult,
                     op1=ALU.subtract,
                 )
-            fold[t, half] = work.tile(grid, F32, tag="fold", name="fold")
+            back = angle[t, half][:, 0, :, :]
             nc.vector.scalar_tensor_tensor(
-                out=fold[t, half][:], in0=back[t, half][:], scalar=-1.0, in1=back[t, half][:], op0=ALU.mult, op1=ALU.min
+                out=angle[t, half][:, 1, :, :], in0=back, scalar=-1.0, in1=back, op0=ALU.mult, op1=ALU.min
             )
 
         def sines(t, half):
             table[t, half] = keep.tile([P, 2, SLOTS, THETAS], F32, name="table%d%d" % (t, half))
             nc.scalar.activation(
-                out=table[t, half][:, 0, :, :], in_=fold[t, half][:], func=ACT.Sin, bias=quarter[:, 0:1], scale=TURN
+                out=table[t, half][:, 0, :, :], in_=angle[t, half][:, 1, :, :], func=ACT.Sin, bias=quarter[:, 0:1], scale=TURN
             )
-            nc.scalar.activation(out=table[t, half][:, 1, :, :], in_=back[t, half][:], func=ACT.Sin, scale=TURN)
+            nc.scalar.activation(out=table[t, half][:, 1, :, :], in_=angle[t, half][:, 0, :, :], func=ACT.Sin, scale=TURN)
 
         def rotate_values(t, half):
             pair = tok[t][:, :, cols(half, 2 * THETAS)].rearrange("p s (i w) -> p w s i", w=2)
@@ -246,7 +248,7 @@ def tile_attentionalsplatting_pb_kernel(
                 for w in range(2):
                     for which in range(2):
                         product[w, which] = work.tile(
-                            [P, SLOTS, PIECE], F32, tag="product%d%d" % (w, which), name="product"
+                            [P, SLOTS, PIECE], F32, tag="product%d%d" % (w, which), name="product", bufs=1
                         )
                         nc.gpsimd.tensor_tensor(
                             out=product[w, which][:],
@@ -283,7 +285,7 @@ def tile_attentionalsplatting_pb_kernel(
 
         def regroup_weights(g, op):
             if op == 0:
-                w_grouped[g] = work.tile([P, D, 2], F32, tag="w_grouped", name="w_grouped", align_bytes=64, bufs=1)
+                w_grouped[g] = work.tile([P, D, 2], F32, tag="angle", name="w_grouped", align_bytes=64)
             nc.scalar.copy(
                 out=w_grouped[g][:, cols(op, 2 * P), :], in_=wt_ps[g, op][:].rearrange("p u ob o -> p (ob o) u")
             )
@@ -337,7 +339,7 @@ def tile_attentionalsplatting_pb_kernel(
         def exponent(m, hh):
             r, hp = divmod(m, DUOS)
             if hp == 0 and hh == 0:
-                rowsum[r] = work.tile([P, H], F32, tag="rowsum", name="rowsum", bufs=6)
+                rowsum[r] = work.tile([P, H], F32, tag="rowsum", name="rowsum", bufs=8)
             if hh == 0:
                 e_of[m] = work.tile([P, 2, M], BF16, tag="e_sb", name="e_sb", bufs=4)
             nc.scalar.activation(
@@ -360,23 +362,26 @@ def tile_attentionalsplatting_pb_kernel(
                     )
 
         def regroup_e(m):
-            eg_of[m] = work.tile([P, 2, P, 2], F32, tag="e_grouped", name="e_grouped", bufs=3, align_bytes=64)
-            nc.scalar.copy(out=eg_of[m][:], in_=et_of[m][:].rearrange("p h u i -> p h i u"))
+            if m % 2 == 0:
+                eg_of[m // 2] = work.tile([P, 4, P, 2], F32, tag="e_grouped", name="e_grouped", align_bytes=64)
+            nc.scalar.copy(
+                out=eg_of[m // 2][:, cols(m % 2, 2), :, :], in_=et_of[m][:].rearrange("p h u i -> p h i u")
+            )
 
-        def quantise_e(m):
-            r, hp = divmod(m, DUOS)
-            if hp == 0:
-                codes[r] = work.tile([P, H * P], U32, tag="e_codes", name="e_codes", align_bytes=64, bufs=3)
-                scales[r] = work.tile([P, H * P], U8, tag="e_scales", name="e_scales", align_bytes=64, bufs=3)
+        def quantise_e(quad):
+            r, half = divmod(quad, 2)
+            if half == 0:
+                codes[r] = work.tile([P, H * P], U32, tag="e_codes", name="e_codes", align_bytes=64, bufs=5)
+                scales[r] = work.tile([P, H * P], U8, tag="e_scales", name="e_scales", align_bytes=64, bufs=5)
             nc.vector.quantize_mx(
-                out=codes[r][:, cols(hp, 2 * P)].bitcast(FP8X4),
-                scales=scales[r][:, cols(hp, 2 * P)],
-                in_=eg_of[m][:].rearrange("p h i u -> p (h i u)").bitcast(BF16),
+                out=codes[r][:, cols(half, 4 * P)].bitcast(FP8X4),
+                scales=scales[r][:, cols(half, 4 * P)],
+                in_=eg_of[quad][:].rearrange("p h i u -> p (h i u)").bitcast(BF16),
             )
 
         def multiply_values(r, half):
             t = r // IT
-            pv[r, half] = psum_m.tile([P, 4, DH], F32, tag="mm", name="pv")
+            pv[r, half] = psum_t.tile([P, 4, DH], F32, tag="tp", name="pv")
             for hq in range(4):
                 h = 4 * half + hq
                 nc.tensor.matmul_mx(
@@ -426,7 +431,7 @@ def tile_attentionalsplatting_pb_kernel(
 
         def project(r, nh):
             s_codes, s_scales = sq_of[r]
-            po[r, nh] = psum_m.tile([P, 512], F32, tag="mm", name="po")
+            po[r, nh] = psum_t.tile([P, 512], F32, tag="tp", name="po")
             for g in range(2):
                 nc.tensor.matmul_mx(
                     out=po[r, nh][:],
@@ -451,15 +456,15 @@ def tile_attentionalsplatting_pb_kernel(
             transpose_key(0, h)
             copy_key(0, h)
         position_terms()
-        transpose_terms(f_terms, f_rows, IT)
-        transpose_terms(t_terms, t_rows, T * JB)
-        angles(0, 0)
-        angles(0, 1)
+        transpose_terms(f_terms, f_rows[:], 1, IT)
+        transpose_terms(t_terms, t_rows[:].rearrange("k t j -> k (t j)"), T, JB)
+        angles(1, 0)
+        angles(1, 1)
         transpose_q(0)
         copy_q(0)
         square_distances(0, 0)
         scale_bias(0, 0)
-        sines(0, 0)
+        sines(1, 0)
         square_distances(0, 1)
         scale_bias(0, 1)
         for h in range(H // 2, H):
@@ -467,13 +472,13 @@ def tile_attentionalsplatting_pb_kernel(
             copy_key(0, h)
         load_k(1)
         load_q(3)
-        sines(0, 1)
-        rotate_values(0, 0)
-        rotate_values(0, 1)
-        for half in range(2):
-            angles(1, half)
-            sines(1, half)
-            rotate_values(1, half)
+        sines(1, 1)
+        for half in (1, 0):
+            angles(0, half)
+            sines(0, half)
+        for t in range(T):
+            for half in range(2):
+                rotate_values(t, half)
         nc.scalar.activation(out=first[:], in_=quarter[:], func=ACT.Exp, scale=1.0)
 
         due = {}
@@ -530,15 +535,16 @@ def tile_attentionalsplatting_pb_kernel(
                 row_shift(n - 1, 1)
             if 0 <= n - 3 < STEPS:
                 regroup_e(n - 3)
+            run(n, normalise, store)
             if 0 <= n - 1 < STEPS:
                 exponent(n - 1, 1)
             run(n, transpose_q, copy_q, load_q, transpose_sampled, regroup_sampled)
-            run(n, transpose_key, copy_key, transpose_weights, regroup_weights)
+            run(n, transpose_key, copy_key, transpose_weights, regroup_weights, square_distances)
             if n < STEPS:
                 begin_scores(n)
                 finish_scores(n)
-            run(n, square_distances, scale_bias, quantise_values)
-            if 0 <= n - 4 < STEPS:
-                quantise_e(n - 4)
-            run(n, normalise, quantise_sampled, quantise_weights, store)
+            run(n, scale_bias, quantise_values)
+            if n % 2 == 1 and 0 <= n - 5 < STEPS:
+                quantise_e((n - 5) // 2)
+            run(n, quantise_sampled, quantise_weights)
             run(n, multiply_values, project)

@@ -34,7 +34,10 @@ PIECE = 128
 SCALE = 1.0 / math.sqrt(DH)
 BIAS_GAIN = 2.0 / SCALE
 TURN = 2.0 * math.pi
-VALUES_STEP = 16
+VALUES_STEP = 19
+VALUES_STEP_1 = 36
+ROTATE_FIRST = 10
+ROTATE_STEADY = 3
 
 FLOPS = 2 * (2 * T * H * HW * M * DH) + 2 * T * HW * D * D
 
@@ -98,11 +101,6 @@ def tile_attentionalsplatting_pb_kernel(
         w_codes = keep.tile([P, 2, D], U32, align_bytes=64)
         w_scales = keep.tile([P, 2, D], U8, align_bytes=64)
 
-        ident_bf = keep.tile([P, P], BF16)
-        ident_f = keep.tile([P, P], F32)
-        make_identity(nc, ident_bf[:])
-        make_identity(nc, ident_f[:])
-
         quarter = keep.tile([P, 1], F32)
         nc.vector.memset(quarter[:], 1.0)
         nc.vector.tensor_scalar_mul(out=quarter[:], in0=quarter[:], scalar1=math.pi / 2.0)
@@ -110,25 +108,30 @@ def tile_attentionalsplatting_pb_kernel(
         nc.scalar.activation(out=first[:], in_=quarter[:], func=ACT.Sin, scale=1.0)
         theta = keep.tile([P, THETAS], F32)
         nc.vector.memset(theta[:, 0:1], 1.0)
-        for doubling in range(8):
-            width = 2**doubling
-            nc.vector.tensor_scalar_mul(
-                out=theta[:, width : 2 * width], in0=theta[:, 0:width], scalar1=100.0 ** (-width / THETAS)
-            )
+        for width in (1, 4, 16, 64):
+            for k in range(1, 4):
+                nc.vector.tensor_scalar_mul(
+                    out=theta[:, cols(k, width)], in0=theta[:, 0:width], scalar1=100.0 ** (-k * width / THETAS)
+                )
+        TERMS = 5
+        f_terms = keep.tile([P, IT, P], BF16)
+        t_terms = keep.tile([P, T * JB, P], BF16)
+        for terms in (f_terms, t_terms):
+            nc.vector.memset(terms[:], 0.0)
+            nc.vector.memset(terms[:, :, 0 : 2 * TERMS], 1.0)
+
+        ident_bf = keep.tile([P, P], BF16)
+        ident_f = keep.tile([P, P], F32)
+        make_identity(nc, ident_bf[:])
+        make_identity(nc, ident_f[:])
+
         turns = keep.tile([P, T, 2, SLOTS], F32)
         nc.vector.tensor_scalar_mul(
             out=turns[:], in0=trk_v[:].rearrange("p t s c -> p t c s"), scalar1=1.0 / TURN
         )
 
-        TERMS = 5
-        f_terms = keep.tile([P, IT, P], BF16)
-        t_terms = keep.tile([P, T * JB, P], BF16)
         f_rows = keep.tile([P, HW], BF16)
         t_rows = keep.tile([P, T, M], BF16)
-
-        for terms in (f_terms, t_terms):
-            nc.gpsimd.memset(terms[:], 0.0)
-            nc.gpsimd.memset(terms[:, :, 0 : 2 * TERMS], 1.0)
 
         def position_terms():
             square = {}
@@ -190,7 +193,7 @@ def tile_attentionalsplatting_pb_kernel(
 
         def copy_key(t, h):
             target = k_t[t][:, h, :].rearrange("p (jb j) -> p jb j", jb=JB)
-            if t == 0:
+            if t == 0 and h < H // 2:
                 nc.scalar.copy(out=target, in_=kt_ps[t, h][:])
             else:
                 nc.vector.tensor_copy(out=target, in_=kt_ps[t, h][:])
@@ -209,13 +212,13 @@ def tile_attentionalsplatting_pb_kernel(
         angle, table, v_grouped = {}, {}, {}
         grid = [P, SLOTS, THETAS]
 
-        def angles(t, half):
+        def reduce_angles(t, half):
             whole = work.tile(grid, I32, tag="bias", bufs=3)
             for s in range(SLOTS):
                 nc.vector.tensor_scalar(
                     out=whole[:, s, :], in0=theta[:], scalar1=turns[:, t, half, s : s + 1], scalar2=None, op0=ALU.mult
                 )
-            angle[t, half] = work.tile([P, 2, SLOTS, THETAS], F32, tag="angle", name="angle", align_bytes=64)
+            angle[t, half] = work.tile([P, 2, SLOTS, THETAS], F32, tag="angle", name="angle", bufs=3, align_bytes=64)
             for s in range(SLOTS):
                 nc.vector.scalar_tensor_tensor(
                     out=angle[t, half][:, 0, s, :],
@@ -225,6 +228,7 @@ def tile_attentionalsplatting_pb_kernel(
                     op0=ALU.mult,
                     op1=ALU.subtract,
                 )
+        def fold_angles(t, half):
             back = angle[t, half][:, 0, :, :]
             nc.vector.scalar_tensor_tensor(
                 out=angle[t, half][:, 1, :, :], in0=back, scalar=-1.0, in1=back, op0=ALU.mult, op1=ALU.min
@@ -232,37 +236,47 @@ def tile_attentionalsplatting_pb_kernel(
 
         def sines(t, half):
             table[t, half] = keep.tile([P, 2, SLOTS, THETAS], F32, name="table%d%d" % (t, half))
+            nc.scalar.activation(out=table[t, half][:, 1, :, :], in_=angle[t, half][:, 0, :, :], func=ACT.Sin, scale=TURN)
             nc.scalar.activation(
                 out=table[t, half][:, 0, :, :], in_=angle[t, half][:, 1, :, :], func=ACT.Sin, bias=quarter[:, 0:1], scale=TURN
             )
-            nc.scalar.activation(out=table[t, half][:, 1, :, :], in_=angle[t, half][:, 0, :, :], func=ACT.Sin, scale=TURN)
 
-        def rotate_values(t, half):
-            pair = tok[t][:, :, cols(half, 2 * THETAS)].rearrange("p s (i w) -> p w s i", w=2)
-            v_grouped[t, half] = work.tile(
-                [P, THETAS, 2, SLOTS], BF16, tag="v_grouped", name="v_grouped", align_bytes=64
-            )
-            for piece in range(THETAS // PIECE):
+        product = {}
+        PARTS = ((0, 0), (0, 1), (1, 0), (1, 1), (0, None), (1, None))
+        rotation = [
+            (t, half, piece, w, which)
+            for t in range(T)
+            for half in range(2)
+            for piece in range(THETAS // PIECE)
+            for w, which in PARTS
+        ]
+
+        def rotate_values(count):
+            for t, half, piece, w, which in rotation[:count]:
                 part = cols(piece, PIECE)
-                product = {}
-                for w in range(2):
-                    for which in range(2):
-                        product[w, which] = work.tile(
-                            [P, SLOTS, PIECE], F32, tag="product%d%d" % (w, which), name="product", bufs=1
-                        )
-                        nc.gpsimd.tensor_tensor(
-                            out=product[w, which][:],
-                            in0=pair[:, w, :, part],
-                            in1=table[t, half][:, which, :, part],
-                            op=ALU.mult,
-                        )
-                for w, op in ((0, ALU.subtract), (1, ALU.add)):
+                if (piece, w, which) == (0, 0, 0):
+                    v_grouped[t, half] = work.tile(
+                        [P, THETAS, 2, SLOTS], BF16, tag="v_grouped", name="v_grouped", align_bytes=64
+                    )
+                if which is not None:
+                    pair = tok[t][:, :, cols(half, 2 * THETAS)].rearrange("p s (i w) -> p w s i", w=2)
+                    product[w, which] = work.tile(
+                        [P, SLOTS, PIECE], F32, tag="product%d%d" % (w, which), name="product", bufs=1
+                    )
+                    nc.gpsimd.tensor_tensor(
+                        out=product[w, which][:],
+                        in0=pair[:, w, :, part],
+                        in1=table[t, half][:, which, :, part],
+                        op=ALU.mult,
+                    )
+                else:
                     nc.gpsimd.tensor_tensor(
                         out=v_grouped[t, half][:, part, w, :],
                         in0=product[0, w][:].rearrange("p s i -> p i s"),
                         in1=product[1, 1 - w][:].rearrange("p s i -> p i s"),
-                        op=op,
+                        op=ALU.add if w else ALU.subtract,
                     )
+            rotation[:count] = []
 
         def quantise_values(t, half):
             nc.vector.quantize_mx(
@@ -285,7 +299,7 @@ def tile_attentionalsplatting_pb_kernel(
 
         def regroup_weights(g, op):
             if op == 0:
-                w_grouped[g] = work.tile([P, D, 2], F32, tag="angle", name="w_grouped", align_bytes=64)
+                w_grouped[g] = work.tile([P, D, 2], F32, tag="angle", name="w_grouped", bufs=3, align_bytes=64)
             nc.scalar.copy(
                 out=w_grouped[g][:, cols(op, 2 * P), :], in_=wt_ps[g, op][:].rearrange("p u ob o -> p (ob o) u")
             )
@@ -371,8 +385,8 @@ def tile_attentionalsplatting_pb_kernel(
         def quantise_e(quad):
             r, half = divmod(quad, 2)
             if half == 0:
-                codes[r] = work.tile([P, H * P], U32, tag="e_codes", name="e_codes", align_bytes=64, bufs=5)
-                scales[r] = work.tile([P, H * P], U8, tag="e_scales", name="e_scales", align_bytes=64, bufs=5)
+                codes[r] = work.tile([P, H * P], U32, tag="e_codes", name="e_codes", align_bytes=64, bufs=4)
+                scales[r] = work.tile([P, H * P], U8, tag="e_scales", name="e_scales", align_bytes=64, bufs=4)
             nc.vector.quantize_mx(
                 out=codes[r][:, cols(half, 4 * P)].bitcast(FP8X4),
                 scales=scales[r][:, cols(half, 4 * P)],
@@ -396,10 +410,12 @@ def tile_attentionalsplatting_pb_kernel(
 
         inv_sum = {}
 
+        def invert_sums(r):
+            inv_sum[r] = work.tile([P, H], F32, tag="inv_sum", name="inv_sum", bufs=6)
+            nc.vector.reciprocal(out=inv_sum[r][:], in_=rowsum[r][:])
+
         def normalise(r, half):
             if half == 0:
-                inv_sum[r] = work.tile([P, H], F32, tag="inv_sum", name="inv_sum")
-                nc.vector.reciprocal(out=inv_sum[r][:], in_=rowsum[r][:])
                 sampled[r] = work.tile([P, 2, 4, DH], BF16, tag="sampled", name="sampled")
             nc.vector.tensor_tensor(
                 out=sampled[r][:, half, :, :],
@@ -445,7 +461,7 @@ def tile_attentionalsplatting_pb_kernel(
 
         def store(r, nh):
             t, it = divmod(r, IT)
-            o_sb = work.tile([P, 512], F32, tag="o_sb", bufs=3)
+            o_sb = work.tile([P, 512], F32, tag="o_sb", bufs=4)
             if nh == 0:
                 nc.scalar.copy(out=o_sb[:], in_=po[r, nh][:])
             else:
@@ -458,27 +474,24 @@ def tile_attentionalsplatting_pb_kernel(
         position_terms()
         transpose_terms(f_terms, f_rows[:], 1, IT)
         transpose_terms(t_terms, t_rows[:].rearrange("k t j -> k (t j)"), T, JB)
-        angles(1, 0)
-        angles(1, 1)
         transpose_q(0)
-        copy_q(0)
         square_distances(0, 0)
-        scale_bias(0, 0)
-        sines(1, 0)
         square_distances(0, 1)
-        scale_bias(0, 1)
-        for h in range(H // 2, H):
-            transpose_key(0, h)
-            copy_key(0, h)
-        load_k(1)
         load_q(3)
+        reduce_angles(1, 0)
+        copy_q(0)
+        scale_bias(0, 0)
+        reduce_angles(1, 1)
+        fold_angles(1, 0)
+        sines(1, 0)
+        fold_angles(1, 1)
         sines(1, 1)
+        scale_bias(0, 1)
         for half in (1, 0):
-            angles(0, half)
+            reduce_angles(0, half)
+            fold_angles(0, half)
             sines(0, half)
-        for t in range(T):
-            for half in range(2):
-                rotate_values(t, half)
+        rotate_values(ROTATE_FIRST)
         nc.scalar.activation(out=first[:], in_=quarter[:], func=ACT.Exp, scale=1.0)
 
         due = {}
@@ -487,8 +500,9 @@ def tile_attentionalsplatting_pb_kernel(
             due.setdefault(step, []).append((work_on, which))
 
         for r in range(ROUNDS):
-            start = max(DUOS * r + 6, VALUES_STEP + 2 * r)
+            start = max(DUOS * r + 6, VALUES_STEP + 2 * r, VALUES_STEP_1 + 2 * (r - IT) if r >= IT else 0)
             second = start + (2 if start == DUOS * r + 6 else 1)
+            at(DUOS * r + 5, invert_sums, r)
             for half, step in ((0, start), (1, second)):
                 at(step, multiply_values, r, half)
                 at(step + 1, normalise, r, half)
@@ -512,13 +526,17 @@ def tile_attentionalsplatting_pb_kernel(
             for op in range(4):
                 at(4 + 4 * g + op, transpose_weights, g, op)
                 at(4 + 4 * g + op, regroup_weights, g, op)
-            at(8 + 4 * g, quantise_weights, g)
+            at(4 + 4 + 4 * g, quantise_weights, g)
         for h in range(H):
             at(12 + h, transpose_key, 1, h)
             at(12 + h, copy_key, 1, h)
+            if h >= H // 2:
+                at(h // 2 - 1, transpose_key, 0, h)
+                at(h // 2 - 1, copy_key, 0, h)
+        at(3, load_k, 1)
         for half in range(2):
             at(VALUES_STEP - 2 + half, quantise_values, 0, half)
-            at(DUOS * IT + 4 + half, quantise_values, 1, half)
+            at(VALUES_STEP_1 - 2 + half, quantise_values, 1, half)
 
         def run(step, *kinds):
             for kind in kinds:
@@ -538,13 +556,18 @@ def tile_attentionalsplatting_pb_kernel(
             run(n, normalise, store)
             if 0 <= n - 1 < STEPS:
                 exponent(n - 1, 1)
-            run(n, transpose_q, copy_q, load_q, transpose_sampled, regroup_sampled)
+            run(n, transpose_q, copy_q, load_q, load_k, transpose_sampled, regroup_sampled)
             run(n, transpose_key, copy_key, transpose_weights, regroup_weights, square_distances)
             if n < STEPS:
                 begin_scores(n)
                 finish_scores(n)
-            run(n, scale_bias, quantise_values)
+            run(n, invert_sums, scale_bias, quantise_values)
             if n % 2 == 1 and 0 <= n - 5 < STEPS:
                 quantise_e((n - 5) // 2)
+                if rotation:
+                    gate = work.tile([P, 1], U32, tag="gate", bufs=1)
+                    r, half = divmod((n - 5) // 2, 2)
+                    nc.gpsimd.tensor_copy(out=gate[:], in_=codes[r][:, (4 * half + 3) * P : (4 * half + 3) * P + 1])
+                    rotate_values(ROTATE_STEADY)
             run(n, quantise_sampled, quantise_weights)
             run(n, multiply_values, project)

@@ -108,22 +108,29 @@ def tile_attentionalsplatting_pb_kernel(
         nc.scalar.activation(out=first[:], in_=quarter[:], func=ACT.Sin, scale=1.0)
         theta = keep.tile([P, THETAS], F32)
         nc.vector.memset(theta[:, 0:1], 1.0)
-        for width in (1, 4, 16, 64):
+
+        def widen_theta(width):
             for k in range(1, 4):
                 nc.vector.tensor_scalar_mul(
                     out=theta[:, cols(k, width)], in0=theta[:, 0:width], scalar1=100.0 ** (-k * width / THETAS)
                 )
+
         TERMS = 5
         f_terms = keep.tile([P, IT, P], BF16)
         t_terms = keep.tile([P, T * JB, P], BF16)
-        for terms in (f_terms, t_terms):
-            nc.vector.memset(terms[:], 0.0)
-            nc.vector.memset(terms[:, :, 0 : 2 * TERMS], 1.0)
+        nc.vector.memset(f_terms[:], 0.0)
+        widen_theta(1)
+        nc.vector.memset(t_terms[:], 0.0)
+        widen_theta(4)
+        nc.vector.memset(f_terms[:, :, 0 : 2 * TERMS], 1.0)
+        widen_theta(16)
+        nc.vector.memset(t_terms[:, :, 0 : 2 * TERMS], 1.0)
+        widen_theta(64)
 
         ident_bf = keep.tile([P, P], BF16)
         ident_f = keep.tile([P, P], F32)
         make_identity(nc, ident_bf[:])
-        make_identity(nc, ident_f[:])
+        nc.vector.tensor_copy(out=ident_f[:], in_=ident_bf[:])
 
         turns = keep.tile([P, T, 2, SLOTS], F32)
         nc.vector.tensor_scalar_mul(

@@ -321,28 +321,26 @@ def tile_attentionalsplatting_pb_kernel(
         score, shift, e_of, et_of, eg_of = {}, {}, {}, {}, {}
         rowsum, codes, scales, pv, sampled, st_of, sg_of, sq_of, po, o_sb = {}, {}, {}, {}, {}, {}, {}, {}, {}, {}
 
-        def begin_scores(m):
+        def begin_scores(m, hh):
             r = m // DUOS
             chunk, part = divmod(r * P, CHUNK)
-            for hh in range(2):
-                score[m, hh] = psum_s.tile([P, M], F32, tag="sc", name="sc")
-                for jb in range(JB):
-                    nc.tensor.matmul(
-                        out=score[m, hh][:, cols(jb, P)],
-                        lhsT=bias[chunk][:, jb, part : part + P],
-                        rhs=ident_f[:],
-                        is_transpose=True,
-                        start=(jb == 0),
-                        stop=False,
-                    )
-
-        def finish_scores(m):
-            r, hp = divmod(m, DUOS)
-            for hh in range(2):
-                h = 2 * hp + hh
+            score[m, hh] = psum_s.tile([P, M], F32, tag="sc", name="sc")
+            for jb in range(JB):
                 nc.tensor.matmul(
-                    out=score[m, hh][:], lhsT=q_t[r][:, h, :], rhs=k_t[r // IT][:, h, :], start=False, stop=True
+                    out=score[m, hh][:, cols(jb, P)],
+                    lhsT=bias[chunk][:, jb, part : part + P],
+                    rhs=ident_f[:],
+                    is_transpose=True,
+                    start=(jb == 0),
+                    stop=False,
                 )
+
+        def finish_scores(m, hh):
+            r, hp = divmod(m, DUOS)
+            h = 2 * hp + hh
+            nc.tensor.matmul(
+                out=score[m, hh][:], lhsT=q_t[r][:, h, :], rhs=k_t[r // IT][:, h, :], start=False, stop=True
+            )
 
         def row_shift(m, hh):
             shift[m, hh] = work.tile([P, 1], F32, tag="shift", name="shift", bufs=6)
@@ -566,8 +564,9 @@ def tile_attentionalsplatting_pb_kernel(
             run(n, transpose_q, copy_q, load_q, load_k, transpose_sampled, regroup_sampled)
             run(n, transpose_key, copy_key, transpose_weights, regroup_weights, square_distances)
             if n < STEPS:
-                begin_scores(n)
-                finish_scores(n)
+                for hh in range(2):
+                    begin_scores(n, hh)
+                    finish_scores(n, hh)
             run(n, invert_sums, scale_bias, quantise_values)
             if n % 2 == 1 and 0 <= n - 5 < STEPS:
                 quantise_e((n - 5) // 2)

@@ -36,8 +36,8 @@ BIAS_GAIN = 2.0 / SCALE
 TURN = 2.0 * math.pi
 VALUES_STEP = 19
 VALUES_STEP_1 = 36
-ROTATE_FIRST = 10
-ROTATE_STEADY = 3
+ROTATE_FIRST = 5
+ROTATE_STEADY = 2
 
 FLOPS = 2 * (2 * T * H * HW * M * DH) + 2 * T * HW * D * D
 
@@ -249,38 +249,37 @@ def tile_attentionalsplatting_pb_kernel(
             )
 
         product = {}
-        PARTS = ((0, 0), (0, 1), (1, 0), (1, 1), (0, None), (1, None))
         rotation = [
-            (t, half, piece, w, which)
+            (t, half, piece, kind, w)
             for t in range(T)
             for half in range(2)
             for piece in range(THETAS // PIECE)
-            for w, which in PARTS
+            for kind in ("product", "sum")
+            for w in range(2)
         ]
 
         def rotate_values(count):
-            for t, half, piece, w, which in rotation[:count]:
+            for t, half, piece, kind, w in rotation[:count]:
                 part = cols(piece, PIECE)
-                if (piece, w, which) == (0, 0, 0):
+                if (piece, kind, w) == (0, "product", 0):
                     v_grouped[t, half] = work.tile(
                         [P, THETAS, 2, SLOTS], BF16, tag="v_grouped", name="v_grouped", align_bytes=64
                     )
-                if which is not None:
+                if kind == "product":
                     pair = tok[t][:, :, cols(half, 2 * THETAS)].rearrange("p s (i w) -> p w s i", w=2)
-                    product[w, which] = work.tile(
-                        [P, SLOTS, PIECE], F32, tag="product%d%d" % (w, which), name="product", bufs=1
-                    )
+                    shape = [P, 2, SLOTS, PIECE]
+                    product[w] = work.tile(shape, F32, tag="product%d" % w, name="product", bufs=1)
                     nc.gpsimd.tensor_tensor(
-                        out=product[w, which][:],
-                        in0=pair[:, w, :, part],
-                        in1=table[t, half][:, which, :, part],
+                        out=product[w][:],
+                        in0=pair[:, w, :, part].unsqueeze(1).to_broadcast(shape),
+                        in1=table[t, half][:, :, :, part],
                         op=ALU.mult,
                     )
                 else:
                     nc.gpsimd.tensor_tensor(
                         out=v_grouped[t, half][:, part, w, :],
-                        in0=product[0, w][:].rearrange("p s i -> p i s"),
-                        in1=product[1, 1 - w][:].rearrange("p s i -> p i s"),
+                        in0=product[0][:, w, :, :].rearrange("p s i -> p i s"),
+                        in1=product[1][:, 1 - w, :, :].rearrange("p s i -> p i s"),
                         op=ALU.add if w else ALU.subtract,
                     )
             rotation[:count] = []

@@ -557,6 +557,8 @@ def tile_attentionalsplatting_pb_kernel(
                 row_shift(n - 1, 1)
             if 0 <= n - 3 < STEPS:
                 regroup_e(n - 3)
+            if n == STEPS + 3:
+                quantise_e((n - 5) // 2)
             run(n, normalise, store)
             if 0 <= n - 1 < STEPS:
                 exponent(n - 1, 1)
@@ -567,7 +569,7 @@ def tile_attentionalsplatting_pb_kernel(
                     begin_scores(n, hh)
                     finish_scores(n, hh)
             run(n, invert_sums, scale_bias, quantise_values)
-            if n % 2 == 1 and 0 <= n - 5 < STEPS:
+            if n % 2 == 1 and 0 <= n - 5 < STEPS - 2:
                 quantise_e((n - 5) // 2)
                 if rotation:
                     gate = work.tile([P, 1], U32, tag="gate", bufs=1)

@@ -29,15 +29,15 @@ THETAS = 256
 SLOTS = 4
 CHUNK = 256
 CHUNKS = T * HW // CHUNK
-PIECE = 128
+PIECE = 64
 
 SCALE = 1.0 / math.sqrt(DH)
 BIAS_GAIN = 2.0 / SCALE
 TURN = 2.0 * math.pi
-VALUES_STEP = 19
-VALUES_STEP_1 = 36
-ROTATE_FIRST = 5
-ROTATE_STEADY = 2
+VALUES_STEP = 21
+VALUES_STEP_1 = 42
+ROTATE_FIRST = 11
+ROTATE_STEADY = 3
 
 FLOPS = 2 * (2 * T * H * HW * M * DH) + 2 * T * HW * D * D
 
@@ -86,11 +86,15 @@ def tile_attentionalsplatting_pb_kernel(
                 in_=updated_track_tokens[t].rearrange("(u p e) c -> p u (e c)", u=2, p=P),
             )
 
-        w_sb = keep.tile([P, D // P, D], BF16)
+        w_sb = []
         load_k(0)
         load_q(0)
         load_tok(0)
-        nc.sync.dma_start(out=w_sb[:], in_=W_out.rearrange("(ob p) c -> p ob c", p=P))
+        for op in range(4):
+            w_sb.append(work.tile([P, 2, D], BF16, tag="w_sb", name="w_sb", bufs=4))
+            nc.sync.dma_start(
+                out=w_sb[op][:], in_=W_out[cols(op, 2 * P), :].rearrange("(ob p) c -> p ob c", p=P)
+            )
         load_q(1)
         load_tok(1)
         load_q(2)
@@ -299,7 +303,7 @@ def tile_attentionalsplatting_pb_kernel(
                 for ob in range(2):
                     nc.tensor.transpose(
                         out=wt_ps[g, op][:, u, ob, :],
-                        in_=w_sb[:, 2 * op + ob, :].bitcast(F32)[:, cols(2 * g + u, P)],
+                        in_=w_sb[op][:, ob, :].bitcast(F32)[:, cols(2 * g + u, P)],
                         identity=ident_f[:],
                     )
 
@@ -465,12 +469,12 @@ def tile_attentionalsplatting_pb_kernel(
 
         def store(r, nh):
             t, it = divmod(r, IT)
-            o_sb = work.tile([P, 512], F32, tag="o_sb", bufs=4)
             if nh == 0:
-                nc.scalar.copy(out=o_sb[:], in_=po[r, nh][:])
+                o_sb[r] = work.tile([P, 2, 512], F32, tag="w_sb", name="o_sb", bufs=4)
+                nc.scalar.copy(out=o_sb[r][:, nh, :], in_=po[r, nh][:])
             else:
-                nc.vector.tensor_copy(out=o_sb[:], in_=po[r, nh][:])
-            nc.sync.dma_start(out=out[t, cols(it, P), cols(nh, 512)], in_=o_sb[:])
+                nc.vector.tensor_copy(out=o_sb[r][:, nh, :], in_=po[r, nh][:])
+            nc.sync.dma_start(out=out[t, cols(it, P), cols(nh, 512)], in_=o_sb[r][:, nh, :])
 
         for h in range(H // 2):
             transpose_key(0, h)

@@ -34,10 +34,12 @@ PIECE = 64
 SCALE = 1.0 / math.sqrt(DH)
 BIAS_GAIN = 2.0 / SCALE
 TURN = 2.0 * math.pi
-VALUES_STEP = 21
+VALUES_STEP = 23
 VALUES_STEP_1 = 42
-ROTATE_FIRST = 11
+ROTATE_FIRST = 9
 ROTATE_STEADY = 3
+ROTATE_LATE = 4
+CODES = 5
 
 FLOPS = 2 * (2 * T * H * HW * M * DH) + 2 * T * HW * D * D
 
@@ -393,8 +395,8 @@ def tile_attentionalsplatting_pb_kernel(
         def quantise_e(quad):
             r, half = divmod(quad, 2)
             if half == 0:
-                codes[r] = work.tile([P, H * P], U32, tag="e_codes", name="e_codes", align_bytes=64, bufs=4)
-                scales[r] = work.tile([P, H * P], U8, tag="e_scales", name="e_scales", align_bytes=64, bufs=4)
+                codes[r] = work.tile([P, H * P], U32, tag="e_codes", name="e_codes", align_bytes=64, bufs=CODES)
+                scales[r] = work.tile([P, H * P], U8, tag="e_scales", name="e_scales", align_bytes=64, bufs=CODES)
             nc.vector.quantize_mx(
                 out=codes[r][:, cols(half, 4 * P)].bitcast(FP8X4),
                 scales=scales[r][:, cols(half, 4 * P)],
@@ -579,6 +581,6 @@ def tile_attentionalsplatting_pb_kernel(
                     gate = work.tile([P, 1], U32, tag="gate", bufs=1)
                     r, half = divmod((n - 5) // 2, 2)
                     nc.gpsimd.tensor_copy(out=gate[:], in_=codes[r][:, (4 * half + 3) * P : (4 * half + 3) * P + 1])
-                    rotate_values(ROTATE_STEADY)
+                    rotate_values(ROTATE_STEADY if n < VALUES_STEP else ROTATE_LATE)
             run(n, quantise_sampled, quantise_weights)
             run(n, multiply_values, project)

@@ -40,6 +40,14 @@ ROTATE_FIRST = 9
 ROTATE_STEADY = 3
 ROTATE_LATE = 4
 CODES = 5
+LAG = 6
+QS = 3
+P0 = 4
+P1 = 6
+K_FIRST = 10
+B0 = 5
+B1 = 1
+W_FIRST = 4
 
 FLOPS = 2 * (2 * T * H * HW * M * DH) + 2 * T * HW * D * D
 
@@ -312,9 +320,8 @@ def tile_attentionalsplatting_pb_kernel(
         def regroup_weights(g, op):
             if op == 0:
                 w_grouped[g] = work.tile([P, D, 2], F32, tag="angle", name="w_grouped", bufs=3, align_bytes=64)
-            nc.scalar.copy(
-                out=w_grouped[g][:, cols(op, 2 * P), :], in_=wt_ps[g, op][:].rearrange("p u ob o -> p (ob o) u")
-            )
+            copy = nc.scalar.copy if op % 2 else nc.vector.tensor_copy
+            copy(out=w_grouped[g][:, cols(op, 2 * P), :], in_=wt_ps[g, op][:].rearrange("p u ob o -> p (ob o) u"))
 
         def quantise_weights(g):
             nc.vector.quantize_mx(
@@ -510,18 +517,18 @@ def tile_attentionalsplatting_pb_kernel(
             due.setdefault(step, []).append((work_on, which))
 
         for r in range(ROUNDS):
-            start = max(DUOS * r + 6, VALUES_STEP + 2 * r, VALUES_STEP_1 + 2 * (r - IT) if r >= IT else 0)
-            second = start + (2 if start == DUOS * r + 6 else 1)
+            start = max(DUOS * r + LAG, VALUES_STEP + 2 * r, VALUES_STEP_1 + 2 * (r - IT) if r >= IT else 0)
+            second = start + (2 if start == DUOS * r + LAG else 1)
             at(DUOS * r + 5, invert_sums, r)
             for half, step in ((0, start), (1, second)):
                 at(step, multiply_values, r, half)
                 at(step + 1, normalise, r, half)
             at(second + 2, transpose_sampled, r)
             at(second + 2, regroup_sampled, r)
-            at(second + 3, quantise_sampled, r)
+            at(second + QS, quantise_sampled, r)
             last = r == ROUNDS - 1
             steady = second == start + 2
-            for nh, step in ((0, second + (4 if last else 5)), (1, second + (4 if last else 7 if steady else 6))):
+            for nh, step in ((0, second + (4 if last else P0)), (1, second + (4 if last else P1 if steady else P0 + 1))):
                 at(step, project, r, nh)
                 at(step + 1, store, r, nh)
             if r + 1 < ROUNDS:
@@ -530,16 +537,16 @@ def tile_attentionalsplatting_pb_kernel(
                 at(DUOS * r + 1, load_q, r + 4)
         for chunk in range(1, CHUNKS):
             for pair in range(2):
-                at(8 * chunk - 5 + 2 * pair, square_distances, chunk, pair)
-                at(8 * chunk - 5 + 2 * pair, scale_bias, chunk, pair)
+                at(8 * chunk - B0 + B1 * pair, square_distances, chunk, pair)
+                at(8 * chunk - B0 + B1 * pair, scale_bias, chunk, pair)
         for g in range(2):
             for op in range(4):
-                at(4 + 4 * g + op, transpose_weights, g, op)
-                at(4 + 4 * g + op, regroup_weights, g, op)
-            at(4 + 4 + 4 * g, quantise_weights, g)
+                at(W_FIRST + 2 * (4 * g + op), transpose_weights, g, op)
+                at(W_FIRST + 2 * (4 * g + op), regroup_weights, g, op)
+            at(W_FIRST + 9 + 8 * g, quantise_weights, g)
         for h in range(H):
-            at(12 + h, transpose_key, 1, h)
-            at(12 + h, copy_key, 1, h)
+            at(K_FIRST + h, transpose_key, 1, h)
+            at(K_FIRST + h, copy_key, 1, h)
             if h >= H // 2:
                 at(h // 2 - 1, transpose_key, 0, h)
                 at(h // 2 - 1, copy_key, 0, h)
@@ -557,24 +564,24 @@ def tile_attentionalsplatting_pb_kernel(
         for n in range(max(due) + 1):
             if 0 <= n - 3 < STEPS:
                 transpose_e(n - 3)
+            run(n, transpose_key, transpose_weights, square_distances, transpose_q, transpose_sampled)
             if 0 <= n - 1 < STEPS:
                 row_shift(n - 1, 0)
-                exponent(n - 1, 0)
+            run(n, store)
+            if 0 <= n - 1 < STEPS:
                 row_shift(n - 1, 1)
             if 0 <= n - 3 < STEPS:
                 regroup_e(n - 3)
-            if n == STEPS + 3:
-                quantise_e((n - 5) // 2)
-            run(n, normalise, store)
-            if 0 <= n - 1 < STEPS:
-                exponent(n - 1, 1)
-            run(n, transpose_q, copy_q, load_q, load_k, transpose_sampled, regroup_sampled)
-            run(n, transpose_key, copy_key, transpose_weights, regroup_weights, square_distances)
+            run(n, regroup_weights, regroup_sampled)
             if n < STEPS:
                 for hh in range(2):
                     begin_scores(n, hh)
                     finish_scores(n, hh)
-            run(n, invert_sums, scale_bias, quantise_values)
+            run(n, normalise, copy_key, project, multiply_values, invert_sums, scale_bias)
+            if 0 <= n - 1 < STEPS:
+                exponent(n - 1, 0)
+                exponent(n - 1, 1)
+            run(n, copy_q, load_q, load_k)
             if n % 2 == 1 and 0 <= n - 5 < STEPS - 2:
                 quantise_e((n - 5) // 2)
                 if rotation:
@@ -582,5 +589,6 @@ def tile_attentionalsplatting_pb_kernel(
                     r, half = divmod((n - 5) // 2, 2)
                     nc.gpsimd.tensor_copy(out=gate[:], in_=codes[r][:, (4 * half + 3) * P : (4 * half + 3) * P + 1])
                     rotate_values(ROTATE_STEADY if n < VALUES_STEP else ROTATE_LATE)
-            run(n, quantise_sampled, quantise_weights)
-            run(n, multiply_values, project)
+            run(n, quantise_values, quantise_weights, quantise_sampled)
+            if n == STEPS + 3:
+                quantise_e((n - 5) // 2)

@@ -46,7 +46,7 @@ P0 = 4
 P1 = 6
 K_FIRST = 10
 B0 = 5
-B1 = 1
+B1 = 2
 W_FIRST = 4
 
 FLOPS = 2 * (2 * T * H * HW * M * DH) + 2 * T * HW * D * D
@@ -320,8 +320,7 @@ def tile_attentionalsplatting_pb_kernel(
         def regroup_weights(g, op):
             if op == 0:
                 w_grouped[g] = work.tile([P, D, 2], F32, tag="angle", name="w_grouped", bufs=3, align_bytes=64)
-            copy = nc.scalar.copy if op % 2 else nc.vector.tensor_copy
-            copy(out=w_grouped[g][:, cols(op, 2 * P), :], in_=wt_ps[g, op][:].rearrange("p u ob o -> p (ob o) u"))
+            nc.scalar.copy(out=w_grouped[g][:, cols(op, 2 * P), :], in_=wt_ps[g, op][:].rearrange("p u ob o -> p (ob o) u"))
 
         def quantise_weights(g):
             nc.vector.quantize_mx(
@@ -480,6 +479,7 @@ def tile_attentionalsplatting_pb_kernel(
             t, it = divmod(r, IT)
             if nh == 0:
                 o_sb[r] = work.tile([P, 2, 512], F32, tag="w_sb", name="o_sb", bufs=4)
+            if nh == 0 or r < ROUNDS - 1:
                 nc.scalar.copy(out=o_sb[r][:, nh, :], in_=po[r, nh][:])
             else:
                 nc.vector.tensor_copy(out=o_sb[r][:, nh, :], in_=po[r, nh][:])

@@ -36,10 +36,12 @@ BIAS_GAIN = 2.0 / SCALE
 TURN = 2.0 * math.pi
 VALUES_STEP = 23
 VALUES_STEP_1 = 42
-ROTATE_FIRST = 9
-ROTATE_STEADY = 3
-ROTATE_LATE = 4
+GROUP = 3
+LATE_GROUP = 5
+LATE_FROM = 13
+ROTATE_FIRST = 3
 CODES = 5
+SHARE = 2
 LAG = 6
 QS = 3
 P0 = 4
@@ -262,43 +264,59 @@ def tile_attentionalsplatting_pb_kernel(
                 out=table[t, half][:, 0, :, :], in_=angle[t, half][:, 1, :, :], func=ACT.Sin, bias=quarter[:, 0:1], scale=TURN
             )
 
-        product = {}
-        rotation = [
-            (t, half, piece, kind, w)
-            for t in range(T)
-            for half in range(2)
-            for piece in range(THETAS // PIECE)
-            for kind in ("product", "sum")
-            for w in range(2)
-        ]
+        products = [keep.tile([P, 2, 2, SLOTS, PIECE], F32, name="products%d" % w) for w in range(2)]
+
+        def rotation_groups():
+            pieces = T * 2 * THETAS // PIECE
+            todo = [(piece, w) for piece in range(pieces) for w in range(2)]
+            ready, groups = [], []
+            while todo or ready:
+                group = []
+                while len(group) < (GROUP if len(groups) < LATE_FROM else LATE_GROUP) and (todo or ready):
+                    if todo and (not group or not ready):
+                        group.append(("product", *todo.pop(0)))
+                        if group[-1][2] == 1:
+                            ready += [(group[-1][1], 0), (group[-1][1], 1)]
+                    else:
+                        group.append(("sum", *ready.pop(0)))
+                groups.append(group)
+            return groups
+
+        rotation = rotation_groups()
 
         def rotate_values(count):
-            for t, half, piece, kind, w in rotation[:count]:
-                part = cols(piece, PIECE)
+            for kind, index, w in [entry for group in rotation[:count] for entry in group]:
+                t, half, piece = index // (2 * THETAS // PIECE), index // (THETAS // PIECE) % 2, index % (THETAS // PIECE)
+                part, place = cols(piece, PIECE), index % 2
                 if (piece, kind, w) == (0, "product", 0):
                     v_grouped[t, half] = work.tile(
                         [P, THETAS, 2, SLOTS], BF16, tag="v_grouped", name="v_grouped", align_bytes=64
                     )
                 if kind == "product":
                     pair = tok[t][:, :, cols(half, 2 * THETAS)].rearrange("p s (i w) -> p w s i", w=2)
-                    shape = [P, 2, SLOTS, PIECE]
-                    product[w] = work.tile(shape, F32, tag="product%d" % w, name="product", bufs=1)
                     nc.gpsimd.tensor_tensor(
-                        out=product[w][:],
-                        in0=pair[:, w, :, part].unsqueeze(1).to_broadcast(shape),
+                        out=products[w][:, place, :, :, :],
+                        in0=pair[:, w, :, part].unsqueeze(1).to_broadcast([P, 2, SLOTS, PIECE]),
                         in1=table[t, half][:, :, :, part],
                         op=ALU.mult,
                     )
                 else:
                     nc.gpsimd.tensor_tensor(
                         out=v_grouped[t, half][:, part, w, :],
-                        in0=product[0][:, w, :, :].rearrange("p s i -> p i s"),
-                        in1=product[1][:, 1 - w, :, :].rearrange("p s i -> p i s"),
+                        in0=products[0][:, place, w, :, :].rearrange("p s i -> p i s"),
+                        in1=products[1][:, place, 1 - w, :, :].rearrange("p s i -> p i s"),
                         op=ALU.add if w else ALU.subtract,
                     )
             rotation[:count] = []
 
+        def hold_rotation():
+            if rotation:
+                kind, index, w = rotation[0][0]
+                gate = work.tile([P, 1], F32, tag="gate", name="gate", bufs=1)
+                nc.vector.tensor_copy(out=gate[:], in_=products[w][:, index % 2, 0, 0, 0:1])
+
         def quantise_values(t, half):
+            assert not [e for gr in rotation for e in gr if e[1] // (THETAS // PIECE) <= 2 * t + half]
             nc.vector.quantize_mx(
                 out=v_codes[t][:, cols(half, 2 * THETAS)].bitcast(FP8X4),
                 scales=v_scales[t][:, cols(half, 2 * THETAS)],
@@ -479,7 +497,7 @@ def tile_attentionalsplatting_pb_kernel(
             t, it = divmod(r, IT)
             if nh == 0:
                 o_sb[r] = work.tile([P, 2, 512], F32, tag="w_sb", name="o_sb", bufs=4)
-            if nh == 0 or r < ROUNDS - 1:
+            if nh == 0 or r % SHARE:
                 nc.scalar.copy(out=o_sb[r][:, nh, :], in_=po[r, nh][:])
             else:
                 nc.vector.tensor_copy(out=o_sb[r][:, nh, :], in_=po[r, nh][:])
@@ -585,10 +603,8 @@ def tile_attentionalsplatting_pb_kernel(
             if n % 2 == 1 and 0 <= n - 5 < STEPS - 2:
                 quantise_e((n - 5) // 2)
                 if rotation:
-                    gate = work.tile([P, 1], U32, tag="gate", bufs=1)
-                    r, half = divmod((n - 5) // 2, 2)
-                    nc.gpsimd.tensor_copy(out=gate[:], in_=codes[r][:, (4 * half + 3) * P : (4 * half + 3) * P + 1])
-                    rotate_values(ROTATE_STEADY if n < VALUES_STEP else ROTATE_LATE)
+                    hold_rotation()
+                    rotate_values(1)
             run(n, quantise_values, quantise_weights, quantise_sampled)
             if n == STEPS + 3:
                 quantise_e((n - 5) // 2)

@@ -34,11 +34,9 @@ PIECE = 64
 SCALE = 1.0 / math.sqrt(DH)
 BIAS_GAIN = 2.0 / SCALE
 TURN = 2.0 * math.pi
-VALUES_STEP = 23
+VALUES_STEP = 21
 VALUES_STEP_1 = 42
-GROUP = 3
-LATE_GROUP = 5
-LATE_FROM = 13
+PACE = (3, 4)
 ROTATE_FIRST = 3
 CODES = 5
 SHARE = 2
@@ -266,57 +264,47 @@ def tile_attentionalsplatting_pb_kernel(
 
         products = [keep.tile([P, 2, 2, SLOTS, PIECE], F32, name="products%d" % w) for w in range(2)]
 
-        def rotation_groups():
-            pieces = T * 2 * THETAS // PIECE
-            todo = [(piece, w) for piece in range(pieces) for w in range(2)]
-            ready, groups = [], []
-            while todo or ready:
-                group = []
-                while len(group) < (GROUP if len(groups) < LATE_FROM else LATE_GROUP) and (todo or ready):
-                    if todo and (not group or not ready):
-                        group.append(("product", *todo.pop(0)))
-                        if group[-1][2] == 1:
-                            ready += [(group[-1][1], 0), (group[-1][1], 1)]
-                    else:
-                        group.append(("sum", *ready.pop(0)))
-                groups.append(group)
-            return groups
+        pieces = list(range(T * 2 * THETAS // PIECE))
 
-        rotation = rotation_groups()
-
-        def rotate_values(count):
-            for kind, index, w in [entry for group in rotation[:count] for entry in group]:
-                t, half, piece = index // (2 * THETAS // PIECE), index // (THETAS // PIECE) % 2, index % (THETAS // PIECE)
-                part, place = cols(piece, PIECE), index % 2
-                if (piece, kind, w) == (0, "product", 0):
-                    v_grouped[t, half] = work.tile(
-                        [P, THETAS, 2, SLOTS], BF16, tag="v_grouped", name="v_grouped", align_bytes=64
-                    )
+        def rotate(engine, index, steps):
+            t, half, piece = index // (2 * THETAS // PIECE), index // (THETAS // PIECE) % 2, index % (THETAS // PIECE)
+            part, place = cols(piece, PIECE), index % 2
+            if (t, half) not in v_grouped:
+                v_grouped[t, half] = work.tile(
+                    [P, THETAS, 2, SLOTS], BF16, tag="v_grouped", name="v_grouped", align_bytes=64
+                )
+            for kind, w in steps:
                 if kind == "product":
                     pair = tok[t][:, :, cols(half, 2 * THETAS)].rearrange("p s (i w) -> p w s i", w=2)
-                    nc.gpsimd.tensor_tensor(
+                    engine.tensor_tensor(
                         out=products[w][:, place, :, :, :],
                         in0=pair[:, w, :, part].unsqueeze(1).to_broadcast([P, 2, SLOTS, PIECE]),
                         in1=table[t, half][:, :, :, part],
                         op=ALU.mult,
                     )
                 else:
-                    nc.gpsimd.tensor_tensor(
+                    engine.tensor_tensor(
                         out=v_grouped[t, half][:, part, w, :],
                         in0=products[0][:, place, w, :, :].rearrange("p s i -> p i s"),
                         in1=products[1][:, place, 1 - w, :, :].rearrange("p s i -> p i s"),
                         op=ALU.add if w else ALU.subtract,
                     )
-            rotation[:count] = []
 
-        def hold_rotation():
-            if rotation:
-                kind, index, w = rotation[0][0]
-                gate = work.tile([P, 1], F32, tag="gate", name="gate", bufs=1)
-                nc.vector.tensor_copy(out=gate[:], in_=products[w][:, index % 2, 0, 0, 0:1])
+        def rotate_alone(count):
+            for index in pieces[:count]:
+                rotate(nc.gpsimd, index, (("product", 0), ("product", 1), ("sum", 0), ("sum", 1)))
+            pieces[:count] = []
+            rotate(nc.gpsimd, pieces[0], (("product", 0),))
+
+        def rotate_together():
+            index = pieces.pop(0)
+            rotate(nc.vector, index, (("product", 1),))
+            rotate(nc.gpsimd, index, (("sum", 0), ("sum", 1)))
+            if pieces:
+                rotate(nc.gpsimd, pieces[0], (("product", 0),))
 
         def quantise_values(t, half):
-            assert not [e for gr in rotation for e in gr if e[1] // (THETAS // PIECE) <= 2 * t + half]
+            assert not [e for e in pieces if e // (THETAS // PIECE) <= 2 * t + half]
             nc.vector.quantize_mx(
                 out=v_codes[t][:, cols(half, 2 * THETAS)].bitcast(FP8X4),
                 scales=v_scales[t][:, cols(half, 2 * THETAS)],
@@ -526,7 +514,7 @@ def tile_attentionalsplatting_pb_kernel(
             reduce_angles(0, half)
             fold_angles(0, half)
             sines(0, half)
-        rotate_values(ROTATE_FIRST)
+        rotate_alone(ROTATE_FIRST)
         nc.scalar.activation(out=first[:], in_=quarter[:], func=ACT.Exp, scale=1.0)
 
         due = {}
@@ -602,9 +590,8 @@ def tile_attentionalsplatting_pb_kernel(
             run(n, copy_q, load_q, load_k)
             if n % 2 == 1 and 0 <= n - 5 < STEPS - 2:
                 quantise_e((n - 5) // 2)
-                if rotation:
-                    hold_rotation()
-                    rotate_values(1)
+                if pieces and (n // 2) % PACE[1] < PACE[0]:
+                    rotate_together()
             run(n, quantise_values, quantise_weights, quantise_sampled)
             if n == STEPS + 3:
                 quantise_e((n - 5) // 2)

import math
from contextlib import ExitStack

import concourse.mybir as mybir
from concourse.masks import make_identity

F32 = mybir.dt.float32
BF16 = mybir.dt.bfloat16
I32 = mybir.dt.int32
U32 = mybir.dt.uint32
U8 = mybir.dt.uint8
FP8X4 = mybir.dt.float8_e4m3fn_x4
ALU = mybir.AluOpType
ACT = mybir.ActivationFunctionType

P = 128
T = 2
M = 512
HW = 768
D = 1024
H = 8
DH = D // H
IT = HW // P
JB = M // P
ROUNDS = T * IT
DUOS = H // 2
STEPS = ROUNDS * DUOS
THETAS = 256
SLOTS = 4
CHUNK = 256
CHUNKS = T * HW // CHUNK
PIECE = 64

SCALE = 1.0 / math.sqrt(DH)
BIAS_GAIN = 2.0 / SCALE
TURN = 2.0 * math.pi
VALUES_STEP = 21
VALUES_STEP_1 = 42
PACE = (3, 4)
ROTATE_FIRST = 3
CODES = 5
SHARE = 2
LAG = 6
QS = 3
P0 = 4
P1 = 6
K_FIRST = 10
B0 = 5
B1 = 2
W_FIRST = 4

FLOPS = 2 * (2 * T * H * HW * M * DH) + 2 * T * HW * D * D


def cols(index, width):
    return slice(index * width, (index + 1) * width)


def tile_attentionalsplatting_pb_kernel(
    tc, q_norm, k_norm, updated_track_tokens, tracks, feature_positions, W_out, out
):
    nc = tc.nc
    with ExitStack() as stack:
        stack.enter_context(tc.manual_schedule())
        keep = stack.enter_context(tc.tile_pool(name="keep", bufs=1))
        work = stack.enter_context(tc.tile_pool(name="work", bufs=2))
        psum_s = stack.enter_context(tc.psum_pool(name="psum_s", bufs=4))
        psum_t = stack.enter_context(tc.psum_pool(name="psum_t", bufs=4))

        trk_p = keep.tile([P, T, JB, 2], BF16)
        trk_v = keep.tile([P, T, SLOTS, 2], BF16)
        fpos = keep.tile([P, IT, 2], BF16)
        with nc.allow_non_contiguous_dma(reason="a few KiB of positions"):
            nc.scalar.dma_start(
                out=trk_v[:].rearrange("p t (u e) c -> p (t u) (e c)", u=2),
                in_=tracks.rearrange("t (u p e) c -> p (t u) (e c)", u=2, p=P),
            )
            nc.sync.dma_start(out=fpos[:], in_=feature_positions.rearrange("(p n) c -> p n c", p=P))
            nc.sync.dma_start(out=trk_p[:], in_=tracks.rearrange("t (p n) c -> p t n c", p=P))

        q_sb, k_sb, tok, q_t = {}, {}, {}, {}

        def load_q(r):
            if r < ROUNDS:
                q_sb[r] = work.tile([P, D], BF16, tag="q_sb", name="q_sb", bufs=3)
                nc.sync.dma_start(out=q_sb[r][:], in_=q_norm[r // IT, cols(r % IT, P), :])

        def load_k(t):
            k_sb[t] = keep.tile([P, JB, D], BF16, tag="k_sb", name="k_sb")
            nc.sync.dma_start(out=k_sb[t][:], in_=k_norm[t].rearrange("(jb p) c -> p jb c", p=P))

        def load_tok(t):
            tok[t] = keep.tile([P, SLOTS, D], BF16, name="tok%d" % t)
            nc.sync.dma_start(
                out=tok[t][:].rearrange("p (u e) c -> p u (e c)", u=2),
                in_=updated_track_tokens[t].rearrange("(u p e) c -> p u (e c)", u=2, p=P),
            )

        w_sb = []
        load_k(0)
        load_q(0)
        load_tok(0)
        for op in range(4):
            w_sb.append(work.tile([P, 2, D], BF16, tag="w_sb", name="w_sb", bufs=4))
            nc.sync.dma_start(
                out=w_sb[op][:], in_=W_out[cols(op, 2 * P), :].rearrange("(ob p) c -> p ob c", p=P)
            )
        load_q(1)
        load_tok(1)
        load_q(2)

        k_t = [keep.tile([P, H, M], BF16, name="k_t%d" % t) for t in range(T)]
        v_codes = [keep.tile([P, D], U32, name="v_codes%d" % t, align_bytes=64) for t in range(T)]
        v_scales = [keep.tile([P, D], U8, name="v_scales%d" % t, align_bytes=64) for t in range(T)]
        w_codes = keep.tile([P, 2, D], U32, align_bytes=64)
        w_scales = keep.tile([P, 2, D], U8, align_bytes=64)

        quarter = keep.tile([P, 1], F32)
        nc.vector.memset(quarter[:], 1.0)
        nc.vector.tensor_scalar_mul(out=quarter[:], in0=quarter[:], scalar1=math.pi / 2.0)
        first = keep.tile([P, 1], F32)
        nc.scalar.activation(out=first[:], in_=quarter[:], func=ACT.Sin, scale=1.0)
        theta = keep.tile([P, THETAS], F32)
        nc.vector.memset(theta[:, 0:1], 1.0)

        def widen_theta(width):
            for k in range(1, 4):
                nc.vector.tensor_scalar_mul(
                    out=theta[:, cols(k, width)], in0=theta[:, 0:width], scalar1=100.0 ** (-k * width / THETAS)
                )

        TERMS = 5
        f_terms = keep.tile([P, IT, P], BF16)
        t_terms = keep.tile([P, T * JB, P], BF16)
        nc.vector.memset(f_terms[:], 0.0)
        widen_theta(1)
        nc.vector.memset(t_terms[:], 0.0)
        widen_theta(4)
        nc.vector.memset(f_terms[:, :, 0 : 2 * TERMS], 1.0)
        widen_theta(16)
        nc.vector.memset(t_terms[:, :, 0 : 2 * TERMS], 1.0)
        widen_theta(64)

        ident_bf = keep.tile([P, P], BF16)
        ident_f = keep.tile([P, P], F32)
        make_identity(nc, ident_bf[:])
        nc.vector.tensor_copy(out=ident_f[:], in_=ident_bf[:])

        turns = keep.tile([P, T, 2, SLOTS], F32)
        nc.vector.tensor_scalar_mul(
            out=turns[:], in0=trk_v[:].rearrange("p t s c -> p t c s"), scalar1=1.0 / TURN
        )

        f_rows = keep.tile([P, HW], BF16)
        t_rows = keep.tile([P, T, M], BF16)

        def position_terms():
            square = {}
            for terms, position, square_at, linear_at, factor in (
                (f_terms, fpos[:], 0, 2, -2.0),
                (t_terms, trk_p[:].rearrange("p t n c -> p (t n) c"), 3, 2, 1.0),
            ):
                at_term = terms[:, :, 0 : 2 * TERMS].rearrange("p n (c k) -> p n c k", c=2)
                square[square_at] = (at_term, position, keep.tile(list(position.shape), F32, name="sq%d" % square_at))
                nc.vector.tensor_tensor(out=square[square_at][2][:], in0=position, in1=position, op=ALU.mult)
                nc.vector.tensor_scalar_mul(out=at_term[:, :, :, linear_at], in0=position, scalar1=factor)
            for square_at, (at_term, position, sq) in square.items():
                nc.vector.tensor_copy(out=at_term[:, :, :, square_at], in_=sq[:])
            for square_at, (at_term, position, sq) in square.items():
                nc.vector.tensor_tensor(
                    out=at_term[:, :, :, square_at + 1], in0=sq[:], in1=at_term[:, :, :, square_at], op=ALU.subtract
                )

        def transpose_terms(terms, rows, frames, count):
            rows_ps = psum_t.tile([P, frames * count, P], BF16, tag="tp", name="rows_ps")
            for n in range(frames * count):
                nc.tensor.transpose(out=rows_ps[:, n, :], in_=terms[:, n, :], identity=ident_bf[:])
            nc.scalar.copy(
                out=rows.rearrange("k (t p n) -> k t p n", t=frames, n=count),
                in_=rows_ps[:].rearrange("k (t n) p -> k t p n", t=frames),
            )

        d2_ps, bias = {}, {}

        def square_distances(chunk, pair):
            t, part = divmod(chunk * CHUNK, HW)
            d2_ps[chunk, pair] = psum_t.tile([P, 2, CHUNK], F32, tag="tp", name="d2_ps")
            for b in range(2):
                nc.tensor.matmul(
                    out=d2_ps[chunk, pair][:, b, :],
                    lhsT=t_rows[:, t, cols(2 * pair + b, P)],
                    rhs=f_rows[:, part : part + CHUNK],
                    start=True,
                    stop=True,
                )

        def scale_bias(chunk, pair):
            if pair == 0:
                bias[chunk] = work.tile([P, JB, CHUNK], F32, tag="bias", name="bias", bufs=3)
            target = bias[chunk][:, 2 * pair : 2 * pair + 2, :]
            if pair == 0:
                nc.scalar.activation(out=target, in_=d2_ps[chunk, pair][:], func=ACT.Copy, scale=-BIAS_GAIN)
            else:
                nc.vector.tensor_scalar_mul(out=target, in0=d2_ps[chunk, pair][:], scalar1=-BIAS_GAIN)

        kt_ps = {}

        def transpose_key(t, h):
            kt_ps[t, h] = psum_t.tile([P, JB, P], BF16, tag="tp", name="kt_ps")
            for jb in range(JB):
                nc.tensor.transpose(
                    out=kt_ps[t, h][:, jb, :], in_=k_sb[t][:, jb, cols(h, DH)], identity=ident_bf[:]
                )

        def copy_key(t, h):
            target = k_t[t][:, h, :].rearrange("p (jb j) -> p jb j", jb=JB)
            if t == 0 and h < H // 2:
                nc.scalar.copy(out=target, in_=kt_ps[t, h][:])
            else:
                nc.vector.tensor_copy(out=target, in_=kt_ps[t, h][:])

        qt_ps = {}

        def transpose_q(r):
            qt_ps[r] = psum_t.tile([P, H, P], BF16, tag="tp", name="qt_ps")
            for h in range(H):
                nc.tensor.transpose(out=qt_ps[r][:, h, :], in_=q_sb[r][:, cols(h, DH)], identity=ident_bf[:])

        def copy_q(r):
            q_t[r] = work.tile([P, H, P], BF16, tag="q_t", name="q_t")
            nc.scalar.copy(out=q_t[r][:], in_=qt_ps[r][:])

        angle, table, v_grouped = {}, {}, {}
        grid = [P, SLOTS, THETAS]

        def reduce_angles(t, half):
            whole = work.tile(grid, I32, tag="bias", bufs=3)
            for s in range(SLOTS):
                nc.vector.tensor_scalar(
                    out=whole[:, s, :], in0=theta[:], scalar1=turns[:, t, half, s : s + 1], scalar2=None, op0=ALU.mult
                )
            angle[t, half] = work.tile([P, 2, SLOTS, THETAS], F32, tag="angle", name="angle", bufs=3, align_bytes=64)
            for s in range(SLOTS):
                nc.vector.scalar_tensor_tensor(
                    out=angle[t, half][:, 0, s, :],
                    in0=theta[:],
                    scalar=turns[:, t, half, s : s + 1],
                    in1=whole[:, s, :],
                    op0=ALU.mult,
                    op1=ALU.subtract,
                )
        def fold_angles(t, half):
            back = angle[t, half][:, 0, :, :]
            nc.vector.scalar_tensor_tensor(
                out=angle[t, half][:, 1, :, :], in0=back, scalar=-1.0, in1=back, op0=ALU.mult, op1=ALU.min
            )

        def sines(t, half):
            table[t, half] = keep.tile([P, 2, SLOTS, THETAS], F32, name="table%d%d" % (t, half))
            nc.scalar.activation(out=table[t, half][:, 1, :, :], in_=angle[t, half][:, 0, :, :], func=ACT.Sin, scale=TURN)
            nc.scalar.activation(
                out=table[t, half][:, 0, :, :], in_=angle[t, half][:, 1, :, :], func=ACT.Sin, bias=quarter[:, 0:1], scale=TURN
            )

        products = [keep.tile([P, 2, 2, SLOTS, PIECE], F32, name="products%d" % w) for w in range(2)]

        pieces = list(range(T * 2 * THETAS // PIECE))

        def rotate(engine, index, steps):
            t, half, piece = index // (2 * THETAS // PIECE), index // (THETAS // PIECE) % 2, index % (THETAS // PIECE)
            part, place = cols(piece, PIECE), index % 2
            if (t, half) not in v_grouped:
                v_grouped[t, half] = work.tile(
                    [P, THETAS, 2, SLOTS], BF16, tag="v_grouped", name="v_grouped", align_bytes=64
                )
            for kind, w in steps:
                if kind == "product":
                    pair = tok[t][:, :, cols(half, 2 * THETAS)].rearrange("p s (i w) -> p w s i", w=2)
                    engine.tensor_tensor(
                        out=products[w][:, place, :, :, :],
                        in0=pair[:, w, :, part].unsqueeze(1).to_broadcast([P, 2, SLOTS, PIECE]),
                        in1=table[t, half][:, :, :, part],
                        op=ALU.mult,
                    )
                else:
                    engine.tensor_tensor(
                        out=v_grouped[t, half][:, part, w, :],
                        in0=products[0][:, place, w, :, :].rearrange("p s i -> p i s"),
                        in1=products[1][:, place, 1 - w, :, :].rearrange("p s i -> p i s"),
                        op=ALU.add if w else ALU.subtract,
                    )

        def rotate_alone(count):
            for index in pieces[:count]:
                rotate(nc.gpsimd, index, (("product", 0), ("product", 1), ("sum", 0), ("sum", 1)))
            pieces[:count] = []
            rotate(nc.gpsimd, pieces[0], (("product", 0),))

        def rotate_together():
            index = pieces.pop(0)
            rotate(nc.vector, index, (("product", 1),))
            rotate(nc.gpsimd, index, (("sum", 0), ("sum", 1)))
            if pieces:
                rotate(nc.gpsimd, pieces[0], (("product", 0),))

        def quantise_values(t, half):
            assert not [e for e in pieces if e // (THETAS // PIECE) <= 2 * t + half]
            nc.vector.quantize_mx(
                out=v_codes[t][:, cols(half, 2 * THETAS)].bitcast(FP8X4),
                scales=v_scales[t][:, cols(half, 2 * THETAS)],
                in_=v_grouped[t, half][:].rearrange("p i w s -> p (i w s)"),
            )

        w_grouped, wt_ps = {}, {}

        def transpose_weights(g, op):
            wt_ps[g, op] = psum_t.tile([P, 2, 2, P], F32, tag="tp", name="wt_ps")
            for u in range(2):
                for ob in range(2):
                    nc.tensor.transpose(
                        out=wt_ps[g, op][:, u, ob, :],
                        in_=w_sb[op][:, ob, :].bitcast(F32)[:, cols(2 * g + u, P)],
                        identity=ident_f[:],
                    )

        def regroup_weights(g, op):
            if op == 0:
                w_grouped[g] = work.tile([P, D, 2], F32, tag="angle", name="w_grouped", bufs=3, align_bytes=64)
            nc.scalar.copy(out=w_grouped[g][:, cols(op, 2 * P), :], in_=wt_ps[g, op][:].rearrange("p u ob o -> p (ob o) u"))

        def quantise_weights(g):
            nc.vector.quantize_mx(
                out=w_codes[:, g, :].bitcast(FP8X4),
                scales=w_scales[:, g, :],
                in_=w_grouped[g][:].rearrange("p o u -> p (o u)").bitcast(BF16),
            )

        score, shift, e_of, et_of, eg_of = {}, {}, {}, {}, {}
        rowsum, codes, scales, pv, sampled, st_of, sg_of, sq_of, po, o_sb = {}, {}, {}, {}, {}, {}, {}, {}, {}, {}

        def begin_scores(m, hh):
            r = m // DUOS
            chunk, part = divmod(r * P, CHUNK)
            score[m, hh] = psum_s.tile([P, M], F32, tag="sc", name="sc")
            for jb in range(JB):
                nc.tensor.matmul(
                    out=score[m, hh][:, cols(jb, P)],
                    lhsT=bias[chunk][:, jb, part : part + P],
                    rhs=ident_f[:],
                    is_transpose=True,
                    start=(jb == 0),
                    stop=False,
                )

        def finish_scores(m, hh):
            r, hp = divmod(m, DUOS)
            h = 2 * hp + hh
            nc.tensor.matmul(
                out=score[m, hh][:], lhsT=q_t[r][:, h, :], rhs=k_t[r // IT][:, h, :], start=False, stop=True
            )

        def row_shift(m, hh):
            shift[m, hh] = work.tile([P, 1], F32, tag="shift", name="shift", bufs=6)
            unread = work.tile([P, M], BF16, tag="unread")
            nc.vector.tensor_scalar(
                out=unread[:],
                in0=score[m, hh][:],
                scalar1=-SCALE,
                scalar2=None,
                op0=ALU.mult,
                op1=ALU.min,
                accum_out=shift[m, hh][:],
            )

        def exponent(m, hh):
            r, hp = divmod(m, DUOS)
            if hp == 0 and hh == 0:
                rowsum[r] = work.tile([P, H], F32, tag="rowsum", name="rowsum", bufs=8)
            if hh == 0:
                e_of[m] = work.tile([P, 2, M], BF16, tag="e_sb", name="e_sb", bufs=4)
            nc.scalar.activation(
                out=e_of[m][:, hh, :],
                in_=score[m, hh][:],
                func=ACT.Exp,
                bias=shift[m, hh][:],
                scale=SCALE,
                accum_out=rowsum[r][:, 2 * hp + hh : 2 * hp + hh + 1],
            )

        def transpose_e(m):
            et_of[m] = psum_t.tile([P, 2, 2, P], F32, tag="tp", name="et_ps")
            for hh in range(2):
                for u in range(2):
                    nc.tensor.transpose(
                        out=et_of[m][:, hh, u, :],
                        in_=e_of[m][:, hh, :].bitcast(F32)[:, cols(u, P)],
                        identity=ident_f[:],
                    )

        def regroup_e(m):
            if m % 2 == 0:
                eg_of[m // 2] = work.tile([P, 4, P, 2], F32, tag="e_grouped", name="e_grouped", align_bytes=64)
            nc.scalar.copy(
                out=eg_of[m // 2][:, cols(m % 2, 2), :, :], in_=et_of[m][:].rearrange("p h u i -> p h i u")
            )

        def quantise_e(quad):
            r, half = divmod(quad, 2)
            if half == 0:
                codes[r] = work.tile([P, H * P], U32, tag="e_codes", name="e_codes", align_bytes=64, bufs=CODES)
                scales[r] = work.tile([P, H * P], U8, tag="e_scales", name="e_scales", align_bytes=64, bufs=CODES)
            nc.vector.quantize_mx(
                out=codes[r][:, cols(half, 4 * P)].bitcast(FP8X4),
                scales=scales[r][:, cols(half, 4 * P)],
                in_=eg_of[quad][:].rearrange("p h i u -> p (h i u)").bitcast(BF16),
            )

        def multiply_values(r, half):
            t = r // IT
            pv[r, half] = psum_t.tile([P, 4, DH], F32, tag="tp", name="pv")
            for hq in range(4):
                h = 4 * half + hq
                nc.tensor.matmul_mx(
                    out=pv[r, half][:, hq, :],
                    lhsT=codes[r][:, cols(h, P)].bitcast(FP8X4),
                    lhsT_scale=scales[r][:, cols(h, P)],
                    rhs=v_codes[t][:, cols(h, DH)].bitcast(FP8X4),
                    rhs_scale=v_scales[t][:, cols(h, DH)],
                    start=True,
                    stop=True,
                )

        inv_sum = {}

        def invert_sums(r):
            inv_sum[r] = work.tile([P, H], F32, tag="inv_sum", name="inv_sum", bufs=6)
            nc.vector.reciprocal(out=inv_sum[r][:], in_=rowsum[r][:])

        def normalise(r, half):
            if half == 0:
                sampled[r] = work.tile([P, 2, 4, DH], BF16, tag="sampled", name="sampled")
            nc.vector.tensor_tensor(
                out=sampled[r][:, half, :, :],
                in0=pv[r, half][:],
                in1=inv_sum[r][:, cols(half, 4)].unsqueeze(2).to_broadcast([P, 4, DH]),
                op=ALU.mult,
            )

        def transpose_sampled(r):
            st_of[r] = psum_t.tile([P, 2, 2, P], F32, tag="tp", name="st_ps")
            words = sampled[r][:].rearrange("p a b c -> p (a b c)").bitcast(F32)
            for g in range(2):
                for u in range(2):
                    nc.tensor.transpose(out=st_of[r][:, g, u, :], in_=words[:, cols(2 * g + u, P)], identity=ident_f[:])

        def regroup_sampled(r):
            sg_of[r] = work.tile([P, 2, P, 2], F32, tag="s_grouped", name="s_grouped", align_bytes=64)
            nc.scalar.copy(out=sg_of[r][:], in_=st_of[r][:].rearrange("p g u i -> p g i u"))

        def quantise_sampled(r):
            s_codes = work.tile([P, 2 * P], U32, tag="s_codes", align_bytes=64, bufs=3)
            s_scales = work.tile([P, 2 * P], U8, tag="s_scales", align_bytes=64, bufs=3)
            nc.vector.quantize_mx(
                out=s_codes[:].bitcast(FP8X4),
                scales=s_scales[:],
                in_=sg_of[r][:].rearrange("p g i u -> p (g i u)").bitcast(BF16),
            )
            sq_of[r] = (s_codes, s_scales)

        def project(r, nh):
            s_codes, s_scales = sq_of[r]
            po[r, nh] = psum_t.tile([P, 512], F32, tag="tp", name="po")
            for g in range(2):
                nc.tensor.matmul_mx(
                    out=po[r, nh][:],
                    lhsT=s_codes[:, cols(g, P)].bitcast(FP8X4),
                    lhsT_scale=s_scales[:, cols(g, P)],
                    rhs=w_codes[:, g, cols(nh, 512)].bitcast(FP8X4),
                    rhs_scale=w_scales[:, g, cols(nh, 512)],
                    start=(g == 0),
                    stop=(g == 1),
                )

        def store(r, nh):
            t, it = divmod(r, IT)
            if nh == 0:
                o_sb[r] = work.tile([P, 2, 512], F32, tag="w_sb", name="o_sb", bufs=4)
            if nh == 0 or r % SHARE:
                nc.scalar.copy(out=o_sb[r][:, nh, :], in_=po[r, nh][:])
            else:
                nc.vector.tensor_copy(out=o_sb[r][:, nh, :], in_=po[r, nh][:])
            nc.sync.dma_start(out=out[t, cols(it, P), cols(nh, 512)], in_=o_sb[r][:, nh, :])

        for h in range(H // 2):
            transpose_key(0, h)
            copy_key(0, h)
        position_terms()
        transpose_terms(f_terms, f_rows[:], 1, IT)
        transpose_terms(t_terms, t_rows[:].rearrange("k t j -> k (t j)"), T, JB)
        transpose_q(0)
        square_distances(0, 0)
        square_distances(0, 1)
        load_q(3)
        reduce_angles(1, 0)
        copy_q(0)
        scale_bias(0, 0)
        reduce_angles(1, 1)
        fold_angles(1, 0)
        sines(1, 0)
        fold_angles(1, 1)
        sines(1, 1)
        scale_bias(0, 1)
        for half in (1, 0):
            reduce_angles(0, half)
            fold_angles(0, half)
            sines(0, half)
        rotate_alone(ROTATE_FIRST)
        nc.scalar.activation(out=first[:], in_=quarter[:], func=ACT.Exp, scale=1.0)

        due = {}

        def at(step, work_on, *which):
            due.setdefault(step, []).append((work_on, which))

        for r in range(ROUNDS):
            start = max(DUOS * r + LAG, VALUES_STEP + 2 * r, VALUES_STEP_1 + 2 * (r - IT) if r >= IT else 0)
            second = start + (2 if start == DUOS * r + LAG else 1)
            at(DUOS * r + 5, invert_sums, r)
            for half, step in ((0, start), (1, second)):
                at(step, multiply_values, r, half)
                at(step + 1, normalise, r, half)
            at(second + 2, transpose_sampled, r)
            at(second + 2, regroup_sampled, r)
            at(second + QS, quantise_sampled, r)
            last = r == ROUNDS - 1
            steady = second == start + 2
            for nh, step in ((0, second + (4 if last else P0)), (1, second + (4 if last else P1 if steady else P0 + 1))):
                at(step, project, r, nh)
                at(step + 1, store, r, nh)
            if r + 1 < ROUNDS:
                at(DUOS * r + 1, transpose_q, r + 1)
                at(DUOS * r + 1, copy_q, r + 1)
                at(DUOS * r + 1, load_q, r + 4)
        for chunk in range(1, CHUNKS):
            for pair in range(2):
                at(8 * chunk - B0 + B1 * pair, square_distances, chunk, pair)
                at(8 * chunk - B0 + B1 * pair, scale_bias, chunk, pair)
        for g in range(2):
            for op in range(4):
                at(W_FIRST + 2 * (4 * g + op), transpose_weights, g, op)
                at(W_FIRST + 2 * (4 * g + op), regroup_weights, g, op)
            at(W_FIRST + 9 + 8 * g, quantise_weights, g)
        for h in range(H):
            at(K_FIRST + h, transpose_key, 1, h)
            at(K_FIRST + h, copy_key, 1, h)
            if h >= H // 2:
                at(h // 2 - 1, transpose_key, 0, h)
                at(h // 2 - 1, copy_key, 0, h)
        at(3, load_k, 1)
        for half in range(2):
            at(VALUES_STEP - 2 + half, quantise_values, 0, half)
            at(VALUES_STEP_1 - 2 + half, quantise_values, 1, half)

        def run(step, *kinds):
            for kind in kinds:
                for work_on, which in due.get(step, []):
                    if work_on == kind:
                        work_on(*which)

        for n in range(max(due) + 1):
            if 0 <= n - 3 < STEPS:
                transpose_e(n - 3)
            run(n, transpose_key, transpose_weights, square_distances, transpose_q, transpose_sampled)
            if 0 <= n - 1 < STEPS:
                row_shift(n - 1, 0)
            run(n, store)
            if 0 <= n - 1 < STEPS:
                row_shift(n - 1, 1)
            if 0 <= n - 3 < STEPS:
                regroup_e(n - 3)
            run(n, regroup_weights, regroup_sampled)
            if n < STEPS:
                for hh in range(2):
                    begin_scores(n, hh)
                    finish_scores(n, hh)
            run(n, normalise, copy_key, project, multiply_values, invert_sums, scale_bias)
            if 0 <= n - 1 < STEPS:
                exponent(n - 1, 0)
                exponent(n - 1, 1)
            run(n, copy_q, load_q, load_k)
            if n % 2 == 1 and 0 <= n - 5 < STEPS - 2:
                quantise_e((n - 5) // 2)
                if pieces and (n // 2) % PACE[1] < PACE[0]:
                    rotate_together()
            run(n, quantise_values, quantise_weights, quantise_sampled)
            if n == STEPS + 3:
                quantise_e((n - 5) // 2)
